import numpy as np
import ml_dtypes


def mxq(x, axis, fmt="e4m3"):
    dtype, down = {"e4m3": (ml_dtypes.float8_e4m3fn, 7), "e5m2": (ml_dtypes.float8_e5m2, 14)}[fmt]
    v = np.moveaxis(np.asarray(x, np.float32).astype(ml_dtypes.bfloat16).astype(np.float64), axis, -1)
    blocks = v.reshape(v.shape[:-1] + (-1, 32))
    amax = np.abs(blocks).max(-1, keepdims=True)
    byte = np.maximum(np.where(amax > 0, np.frexp(amax)[1] - 1 + 127, 0) - down, 1)
    scale = np.exp2(byte - 127.0)
    codes = (blocks / scale).astype(np.float32).astype(dtype).astype(np.float64)
    return np.moveaxis((codes * scale).reshape(v.shape), -1, axis)


WIDE = False


def mx_kscale(k):
    if not WIDE:
        return np.ones(k)
    levels = np.array([10, -10, 5, -5, 0])
    a = np.random.permutation(np.resize(levels, k // 512 * 4)).reshape(k // 512, 4)
    idx = np.arange(k)
    return np.exp2(a[idx // 512, idx % 128 // 32])


BF16 = ml_dtypes.bfloat16


def bf(x):
    return np.asarray(x, np.float32).astype(BF16)


def f64(x):
    return np.asarray(x).astype(np.float64)


N, M, J, DIN, D, G = 1536, 1536, 1536, 256, 128, 2
QS, KC, KN, CS, VS = 1.5, 1.0, 0.2, 1.0, 8.0
EPS = 1e-9


def elu(r):
    return np.where(r > 0.0, r, np.exp(np.minimum(r, 0.0)) - 1.0)


def setup_inputs():
    s = mx_kscale(M)
    g = np.random.randint(G, size=M)
    q = np.random.standard_normal((N, D)) * QS
    q[:, 0] = QS
    k = np.random.standard_normal((G, D))[g] * KC + np.random.standard_normal((M, D)) * KN
    k[:, 0] += np.log(s) * np.sqrt(D) / QS
    profile = np.exp(CS * np.random.standard_normal((G, J)) - CS * CS / 2.0)
    c = profile[g] * (0.75 + 0.5 * np.random.random((M, J))) / s[:, None]
    v = np.random.standard_normal((J, D)) * VS
    return {"q": bf(q), "k": bf(k), "counting_attn": bf(c), "v": bf(v)}


def reference(q, k, counting_attn, v):
    logits = (f64(q) @ f64(k).T) * (1.0 / np.sqrt(D))
    logits = logits - logits.max(axis=1, keepdims=True)
    e = np.exp(logits)
    a_nomi = mxq(e, 1, "e4m3") @ mxq(f64(counting_attn), 0, "e4m3")
    a_deno = a_nomi.sum(axis=1, keepdims=True)
    a_nor = a_nomi / (a_deno + EPS)
    ret = mxq(a_nor, 1, "e4m3") @ mxq(f64(v), 0, "e4m3")
    return elu(ret)

@@ -1,0 +1,240 @@
+from contextlib import ExitStack
+
+import concourse.mybir as mybir
+from concourse.masks import make_identity
+
+F32 = mybir.dt.float32
+BF16 = mybir.dt.bfloat16
+U32 = mybir.dt.uint32
+U8 = mybir.dt.uint8
+FP8X4 = mybir.dt.float8_e4m3fn_x4
+ACT = mybir.ActivationFunctionType
+ALU = mybir.AluOpType
+AX = mybir.AxisListType
+
+P = 128
+PACK = 4
+K_PASS = P * PACK
+NODES = 1536
+D = 128
+TILES = NODES // P
+PASSES = NODES // K_PASS
+BANK = 512
+CHUNKS = NODES // BANK
+AHEAD = 2
+LOGIT_SCALE = 1.0 / (D ** 0.5)
+EPS = 1e-9
+
+FLOPS = 2 * NODES * NODES * D + 2 * NODES * NODES * NODES + 2 * NODES * NODES * D
+
+
+def copy_on(nc, g, out, in_):
+    if g == 0:
+        nc.vector.tensor_copy(out=out, in_=in_)
+    else:
+        nc.scalar.copy(out=out, in_=in_)
+
+
+def turn_and_quantise(nc, sbuf, psum, ident, rows, codes, scales):
+    grouped = sbuf.tile([P, PASSES, P, PACK], BF16, align_bytes=64)
+    for g in range(PASSES):
+        turned = psum.tile([P, PACK, P], BF16)
+        for t in range(PACK):
+            c0 = g * K_PASS + t * P
+            nc.tensor.transpose(turned[:, t, :], rows[:, c0 : c0 + P], ident)
+        copy_on(nc, g, grouped[:, g], turned[:].rearrange("p t r -> p r t"))
+    for g in range(PASSES):
+        nc.vector.quantize_mx(
+            out=codes[:, g, :].bitcast(FP8X4),
+            scales=scales[:, g, :],
+            in_=grouped[:, g].rearrange("p r t -> p (r t)"),
+        )
+
+
+def tile_gkatlayer_pa_kernel(tc, q, k, counting_attn, v, out):
+    nc = tc.nc
+    with ExitStack() as ctx:
+        keep = ctx.enter_context(tc.tile_pool(name="keep", bufs=1))
+        c_in = ctx.enter_context(tc.tile_pool(name="c_in", bufs=PASSES))
+        c_stage = ctx.enter_context(tc.tile_pool(name="c_stage", bufs=3))
+        work = ctx.enter_context(tc.tile_pool(name="work", bufs=3))
+        stage = ctx.enter_context(tc.tile_pool(name="stage", bufs=4))
+        e_keep = ctx.enter_context(tc.tile_pool(name="e_keep", bufs=AHEAD + 2))
+        small = ctx.enter_context(tc.tile_pool(name="small", bufs=4))
+        ps_logits = ctx.enter_context(tc.psum_pool(name="ps_logits", bufs=2))
+        ps_turned = ctx.enter_context(tc.psum_pool(name="ps_turned", bufs=3))
+        ps_sums = ctx.enter_context(tc.psum_pool(name="ps_sums", bufs=2))
+        ps_out = ctx.enter_context(tc.psum_pool(name="ps_out", bufs=1))
+
+        ident = keep.tile([P, P], BF16)
+        make_identity(nc, ident[:])
+
+        k_raw = keep.tile([P, PASSES, PACK, D], BF16)
+        nc.sync.dma_start(out=k_raw[:], in_=k.rearrange("(g p t) d -> p g t d", p=P, t=PACK))
+        q_raw = keep.tile([P, TILES, D], BF16)
+        nc.sync.dma_start(out=q_raw[:], in_=q.rearrange("(p i) d -> p i d", i=TILES))
+        c_raw = []
+        for g in range(PASSES):
+            c_rows = c_in.tile([P, PACK, NODES], BF16)
+            nc.sync.dma_start(
+                out=c_rows[:],
+                in_=counting_attn[g * K_PASS : (g + 1) * K_PASS, :].rearrange("(p t) j -> p t j", t=PACK),
+            )
+            c_raw.append(c_rows)
+        v_raw = keep.tile([P, PASSES, PACK, D], BF16)
+        nc.sync.dma_start(out=v_raw[:], in_=v.rearrange("(g t p) d -> p g t d", t=PACK, p=P))
+
+        kT = keep.tile([P, NODES], BF16)
+        qT = keep.tile([P, NODES], BF16)
+        for g in range(PASSES):
+            turned = ps_turned.tile([P, PACK, P], BF16)
+            for t in range(PACK):
+                nc.tensor.transpose(turned[:, t, :], k_raw[:, g, t, :], ident[:])
+            nc.vector.tensor_copy(out=kT[:, g * K_PASS : (g + 1) * K_PASS], in_=turned[:].rearrange("p t r -> p (t r)"))
+        for g in range(PASSES):
+            turned = ps_turned.tile([P, PACK, P], BF16)
+            for t in range(PACK):
+                nc.tensor.transpose(turned[:, t, :], q_raw[:, g * PACK + t, :], ident[:])
+            nc.scalar.copy(out=qT[:, g * K_PASS : (g + 1) * K_PASS], in_=turned[:].rearrange("p t r -> p (t r)"))
+
+        c_codes = keep.tile([P, PASSES, NODES], U32, align_bytes=64)
+        c_scales = keep.tile([P, PASSES, NODES], U8, align_bytes=64)
+        v_codes = keep.tile([P, PASSES, D], U32, align_bytes=64)
+        v_scales = keep.tile([P, PASSES, D], U8, align_bytes=64)
+        result = keep.tile([P, TILES, D], F32)
+        out_tiles = out.rearrange("(p i) d -> p i d", i=TILES)
+
+        def softmax_numerator(i):
+            scaled = work.tile([P, CHUNKS, BANK], F32)
+            chunk_max = small.tile([P, CHUNKS], F32)
+            for c in range(CHUNKS):
+                logits = ps_logits.tile([P, BANK], F32)
+                nc.tensor.matmul(
+                    out=logits[:],
+                    lhsT=qT[:, i * P : (i + 1) * P],
+                    rhs=kT[:, c * BANK : (c + 1) * BANK],
+                    start=True,
+                    stop=True,
+                )
+                nc.vector.tensor_scalar(
+                    out=scaled[:, c, :],
+                    in0=logits[:],
+                    scalar1=LOGIT_SCALE,
+                    scalar2=None,
+                    op0=ALU.mult,
+                    op1=ALU.max,
+                    accum_out=chunk_max[:, c : c + 1],
+                )
+            minus_max = small.tile([P, 1], F32)
+            nc.vector.tensor_reduce(out=minus_max[:], in_=chunk_max[:], axis=AX.X, op=ALU.max, negate=True)
+            e_rows = work.tile([P, NODES], BF16)
+            nc.scalar.activation(
+                out=e_rows[:],
+                in_=scaled[:].rearrange("p c m -> p (c m)"),
+                func=ACT.Exp,
+                bias=minus_max[:, 0:1],
+                scale=1.0,
+            )
+            e_codes = e_keep.tile([P, PASSES, P], U32, align_bytes=64)
+            e_scales = e_keep.tile([P, PASSES, P], U8, align_bytes=64)
+            turn_and_quantise(nc, stage, ps_turned, ident[:], e_rows, e_codes, e_scales)
+            return e_codes, e_scales
+
+        def quantise_counting_attn(g):
+            for c in range(CHUNKS):
+                c_grouped = c_stage.tile([P, BANK, PACK], BF16, align_bytes=64)
+                dst = c_grouped[:].rearrange("p (w i) t -> p w t i", i=4)
+                src = c_raw[g][:, :, c * BANK : (c + 1) * BANK].rearrange("p t (w i) -> p w t i", i=4)
+                if c == CHUNKS - 1:
+                    nc.scalar.copy(out=dst, in_=src)
+                else:
+                    nc.vector.tensor_copy(out=dst, in_=src)
+                nc.vector.quantize_mx(
+                    out=c_codes[:, g, c * BANK : (c + 1) * BANK].bitcast(FP8X4),
+                    scales=c_scales[:, g, c * BANK : (c + 1) * BANK],
+                    in_=c_grouped[:].rearrange("p w t -> p (w t)"),
+                )
+
+        def quantise_v():
+            v_grouped = keep.tile([P, PASSES, D, PACK], BF16, align_bytes=64)
+            nc.vector.tensor_copy(out=v_grouped[:], in_=v_raw[:].rearrange("p g t d -> p g d t"))
+            for g in range(PASSES):
+                nc.vector.quantize_mx(
+                    out=v_codes[:, g, :].bitcast(FP8X4),
+                    scales=v_scales[:, g, :],
+                    in_=v_grouped[:, g].rearrange("p d t -> p (d t)"),
+                )
+
+        def attend(i, e_codes, e_scales):
+            a_nomi = work.tile([P, CHUNKS, BANK], F32)
+            chunk_sum = small.tile([P, CHUNKS], F32)
+            for c in range(CHUNKS):
+                sums = ps_sums.tile([P, BANK], F32)
+                for g in range(PASSES):
+                    nc.tensor.matmul_mx(
+                        out=sums[:],
+                        lhsT=e_codes[:, g, :].bitcast(FP8X4),
+                        lhsT_scale=e_scales[:, g, :],
+                        rhs=c_codes[:, g, c * BANK : (c + 1) * BANK].bitcast(FP8X4),
+                        rhs_scale=c_scales[:, g, c * BANK : (c + 1) * BANK],
+                        start=(g == 0),
+                        stop=(g == PASSES - 1),
+                    )
+                nc.scalar.activation(
+                    out=a_nomi[:, c, :], in_=sums[:], func=ACT.Copy, accum_out=chunk_sum[:, c : c + 1]
+                )
+            unused = small.tile([P, CHUNKS], F32)
+            a_deno = small.tile([P, 1], F32)
+            nc.vector.tensor_scalar(
+                out=unused[:],
+                in0=chunk_sum[:],
+                scalar1=1.0,
+                scalar2=EPS,
+                op0=ALU.mult,
+                op1=ALU.add,
+                accum_out=a_deno[:],
+            )
+            inverse = small.tile([P, 1], F32)
+            nc.vector.reciprocal(out=inverse[:], in_=a_deno[:])
+            a_nor = work.tile([P, NODES], BF16)
+            nc.vector.tensor_scalar(
+                out=a_nor[:],
+                in0=a_nomi[:].rearrange("p c j -> p (c j)"),
+                scalar1=inverse[:, 0:1],
+                scalar2=None,
+                op0=ALU.mult,
+            )
+            a_codes = stage.tile([P, PASSES, P], U32, align_bytes=64)
+            a_scales = stage.tile([P, PASSES, P], U8, align_bytes=64)
+            turn_and_quantise(nc, stage, ps_turned, ident[:], a_nor, a_codes, a_scales)
+
+            ret = ps_out.tile([P, D], F32)
+            for g in range(PASSES):
+                nc.tensor.matmul_mx(
+                    out=ret[:],
+                    lhsT=a_codes[:, g, :].bitcast(FP8X4),
+                    lhsT_scale=a_scales[:, g, :],
+                    rhs=v_codes[:, g, :].bitcast(FP8X4),
+                    rhs_scale=v_scales[:, g, :],
+                    start=(g == 0),
+                    stop=(g == PASSES - 1),
+                )
+            negative = small.tile([P, D], F32)
+            nc.vector.tensor_scalar_min(out=negative[:], in0=ret[:], scalar1=0.0)
+            grown = small.tile([P, D], F32)
+            nc.scalar.activation(out=grown[:], in_=negative[:], func=ACT.Exp)
+            nc.vector.scalar_tensor_tensor(
+                out=result[:, i, :], in0=grown[:], scalar=-1.0, in1=ret[:], op0=ALU.add, op1=ALU.max
+            )
+            nc.sync.dma_start(out=out_tiles[:, i, :], in_=result[:, i, :])
+
+        quantised_e = []
+        for i in range(AHEAD):
+            quantised_e.append(softmax_numerator(i))
+        for g in range(PASSES):
+            quantise_counting_attn(g)
+        quantise_v()
+        for i in range(TILES):
+            if i + AHEAD < TILES:
+                quantised_e.append(softmax_numerator(i + AHEAD))
+            attend(i, quantised_e[i][0], quantised_e[i][1])

@@ -21,50 +21,24 @@ TILES = NODES // P
 PASSES = NODES // K_PASS
 BANK = 512
 CHUNKS = NODES // BANK
-AHEAD = 2
+HALF = NODES // 2
 LOGIT_SCALE = 1.0 / (D ** 0.5)
 EPS = 1e-9
 
 FLOPS = 2 * NODES * NODES * D + 2 * NODES * NODES * NODES + 2 * NODES * NODES * D
 
 
-def copy_on(nc, g, out, in_):
-    if g == 0:
-        nc.vector.tensor_copy(out=out, in_=in_)
-    else:
-        nc.scalar.copy(out=out, in_=in_)
-
-
-def turn_and_quantise(nc, sbuf, psum, ident, rows, codes, scales):
-    grouped = sbuf.tile([P, PASSES, P, PACK], BF16, align_bytes=64)
-    for g in range(PASSES):
-        turned = psum.tile([P, PACK, P], BF16)
-        for t in range(PACK):
-            c0 = g * K_PASS + t * P
-            nc.tensor.transpose(turned[:, t, :], rows[:, c0 : c0 + P], ident)
-        copy_on(nc, g, grouped[:, g], turned[:].rearrange("p t r -> p r t"))
-    for g in range(PASSES):
-        nc.vector.quantize_mx(
-            out=codes[:, g, :].bitcast(FP8X4),
-            scales=scales[:, g, :],
-            in_=grouped[:, g].rearrange("p r t -> p (r t)"),
-        )
-
-
 def tile_gkatlayer_pa_kernel(tc, q, k, counting_attn, v, out):
     nc = tc.nc
     with ExitStack() as ctx:
+        ctx.enter_context(tc.manual_schedule())
         keep = ctx.enter_context(tc.tile_pool(name="keep", bufs=1))
         c_in = ctx.enter_context(tc.tile_pool(name="c_in", bufs=PASSES))
-        c_stage = ctx.enter_context(tc.tile_pool(name="c_stage", bufs=3))
-        work = ctx.enter_context(tc.tile_pool(name="work", bufs=3))
-        stage = ctx.enter_context(tc.tile_pool(name="stage", bufs=4))
-        e_keep = ctx.enter_context(tc.tile_pool(name="e_keep", bufs=AHEAD + 2))
+        work = ctx.enter_context(tc.tile_pool(name="work", bufs=2))
         small = ctx.enter_context(tc.tile_pool(name="small", bufs=4))
-        ps_logits = ctx.enter_context(tc.psum_pool(name="ps_logits", bufs=2))
+        ps_plain = ctx.enter_context(tc.psum_pool(name="ps_plain", bufs=2))
+        ps_sums = ctx.enter_context(tc.psum_pool(name="ps_sums", bufs=3))
         ps_turned = ctx.enter_context(tc.psum_pool(name="ps_turned", bufs=3))
-        ps_sums = ctx.enter_context(tc.psum_pool(name="ps_sums", bufs=2))
-        ps_out = ctx.enter_context(tc.psum_pool(name="ps_out", bufs=1))
 
         ident = keep.tile([P, P], BF16)
         make_identity(nc, ident[:])
@@ -86,17 +60,6 @@ def tile_gkatlayer_pa_kernel(tc, q, k, counting_attn, v, out):
 
         kT = keep.tile([P, NODES], BF16)
         qT = keep.tile([P, NODES], BF16)
-        for g in range(PASSES):
-            turned = ps_turned.tile([P, PACK, P], BF16)
-            for t in range(PACK):
-                nc.tensor.transpose(turned[:, t, :], k_raw[:, g, t, :], ident[:])
-            nc.vector.tensor_copy(out=kT[:, g * K_PASS : (g + 1) * K_PASS], in_=turned[:].rearrange("p t r -> p (t r)"))
-        for g in range(PASSES):
-            turned = ps_turned.tile([P, PACK, P], BF16)
-            for t in range(PACK):
-                nc.tensor.transpose(turned[:, t, :], q_raw[:, g * PACK + t, :], ident[:])
-            nc.scalar.copy(out=qT[:, g * K_PASS : (g + 1) * K_PASS], in_=turned[:].rearrange("p t r -> p (t r)"))
-
         c_codes = keep.tile([P, PASSES, NODES], U32, align_bytes=64)
         c_scales = keep.tile([P, PASSES, NODES], U8, align_bytes=64)
         v_codes = keep.tile([P, PASSES, D], U32, align_bytes=64)
@@ -104,137 +67,250 @@ def tile_gkatlayer_pa_kernel(tc, q, k, counting_attn, v, out):
         result = keep.tile([P, TILES, D], F32)
         out_tiles = out.rearrange("(p i) d -> p i d", i=TILES)
 
-        def softmax_numerator(i):
-            scaled = work.tile([P, CHUNKS, BANK], F32)
-            chunk_max = small.tile([P, CHUNKS], F32)
-            for c in range(CHUNKS):
-                logits = ps_logits.tile([P, BANK], F32)
-                nc.tensor.matmul(
-                    out=logits[:],
-                    lhsT=qT[:, i * P : (i + 1) * P],
-                    rhs=kT[:, c * BANK : (c + 1) * BANK],
-                    start=True,
-                    stop=True,
-                )
-                nc.vector.tensor_scalar(
-                    out=scaled[:, c, :],
-                    in0=logits[:],
-                    scalar1=LOGIT_SCALE,
-                    scalar2=None,
-                    op0=ALU.mult,
-                    op1=ALU.max,
-                    accum_out=chunk_max[:, c : c + 1],
-                )
-            minus_max = small.tile([P, 1], F32)
-            nc.vector.tensor_reduce(out=minus_max[:], in_=chunk_max[:], axis=AX.X, op=ALU.max, negate=True)
-            e_rows = work.tile([P, NODES], BF16)
+        live = {}
+
+        def four_transposes(blocks):
+            turned = ps_turned.tile([P, PACK, P], BF16, name="turned")
+            for t in range(PACK):
+                nc.tensor.transpose(turned[:, t, :], blocks[t], ident[:])
+            return turned
+
+        def quantise(grouped, codes, scales, g):
+            nc.vector.quantize_mx(
+                out=codes[:, g, :].bitcast(FP8X4),
+                scales=scales[:, g, :],
+                in_=grouped[:, g].rearrange("p r t -> p (r t)"),
+            )
+
+        def logits_chunk(i, c):
+            if c == 0:
+                live["scaled", i] = work.tile([P, CHUNKS, BANK], F32, name="scaled")
+                live["chunk_max", i] = small.tile([P, CHUNKS], F32, name="chunk_max")
+            logits = ps_plain.tile([P, BANK], F32, name="logits", tag="plain")
+            nc.tensor.matmul(
+                out=logits[:],
+                lhsT=qT[:, i * P : (i + 1) * P],
+                rhs=kT[:, c * BANK : (c + 1) * BANK],
+                start=True,
+                stop=True,
+            )
+            nc.vector.tensor_scalar(
+                out=live["scaled", i][:, c, :],
+                in0=logits[:],
+                scalar1=LOGIT_SCALE,
+                scalar2=None,
+                op0=ALU.mult,
+                op1=ALU.max,
+                accum_out=live["chunk_max", i][:, c : c + 1],
+            )
+
+        def row_maximum(i):
+            live["minus_max", i] = small.tile([P, 1], F32, name="minus_max")
+            nc.vector.tensor_reduce(
+                out=live["minus_max", i][:], in_=live["chunk_max", i][:], axis=AX.X, op=ALU.max, negate=True
+            )
+
+        def exponent(i):
+            live["e_rows", i] = work.tile([P, NODES], BF16, name="e_rows")
             nc.scalar.activation(
-                out=e_rows[:],
-                in_=scaled[:].rearrange("p c m -> p (c m)"),
+                out=live["e_rows", i][:],
+                in_=live["scaled", i][:].rearrange("p c m -> p (c m)"),
                 func=ACT.Exp,
-                bias=minus_max[:, 0:1],
+                bias=live["minus_max", i][:, 0:1],
                 scale=1.0,
             )
-            e_codes = e_keep.tile([P, PASSES, P], U32, align_bytes=64)
-            e_scales = e_keep.tile([P, PASSES, P], U8, align_bytes=64)
-            turn_and_quantise(nc, stage, ps_turned, ident[:], e_rows, e_codes, e_scales)
-            return e_codes, e_scales
+
+        def turn_e(i, g):
+            if g == 0:
+                live["e_grouped", i] = work.tile([P, PASSES, P, PACK], BF16, name="e_grouped", align_bytes=64)
+                live["e_codes", i] = work.tile([P, PASSES, P], U32, name="e_codes", bufs=3, align_bytes=64)
+                live["e_scales", i] = work.tile([P, PASSES, P], U8, name="e_scales", bufs=3, align_bytes=64)
+            rows = live["e_rows", i]
+            turned = four_transposes([rows[:, (g * PACK + t) * P : (g * PACK + t + 1) * P] for t in range(PACK)])
+            nc.scalar.copy(out=live["e_grouped", i][:, g], in_=turned[:].rearrange("p t r -> p r t"))
+
+        def counting_chunk(i, c):
+            if c == 0:
+                live["a_nomi", i] = work.tile([P, CHUNKS, BANK], F32, name="a_nomi")
+                live["chunk_sum", i] = small.tile([P, CHUNKS], F32, name="chunk_sum")
+            sums = ps_sums.tile([P, BANK], F32, name="sums")
+            for g in range(PASSES):
+                nc.tensor.matmul_mx(
+                    out=sums[:],
+                    lhsT=live["e_codes", i][:, g, :].bitcast(FP8X4),
+                    lhsT_scale=live["e_scales", i][:, g, :],
+                    rhs=c_codes[:, g, c * BANK : (c + 1) * BANK].bitcast(FP8X4),
+                    rhs_scale=c_scales[:, g, c * BANK : (c + 1) * BANK],
+                    start=(g == 0),
+                    stop=(g == PASSES - 1),
+                )
+            nc.scalar.activation(
+                out=live["a_nomi", i][:, c, :],
+                in_=sums[:],
+                func=ACT.Copy,
+                accum_out=live["chunk_sum", i][:, c : c + 1],
+            )
+
+        def row_sum(i):
+            unused = small.tile([P, CHUNKS], F32, name="unused")
+            live["a_deno", i] = small.tile([P, 1], F32, name="a_deno")
+            nc.vector.tensor_scalar(
+                out=unused[:],
+                in0=live["chunk_sum", i][:],
+                scalar1=1.0,
+                scalar2=EPS,
+                op0=ALU.mult,
+                op1=ALU.add,
+                accum_out=live["a_deno", i][:],
+            )
+
+        def invert(i):
+            live["inverse", i] = small.tile([P, 1], F32, name="inverse")
+            nc.vector.reciprocal(out=live["inverse", i][:], in_=live["a_deno", i][:])
+
+        def normalise(i):
+            live["a_nor", i] = work.tile([P, NODES], BF16, name="a_nor")
+            nc.vector.tensor_scalar(
+                out=live["a_nor", i][:],
+                in0=live["a_nomi", i][:].rearrange("p c j -> p (c j)"),
+                scalar1=live["inverse", i][:, 0:1],
+                scalar2=None,
+                op0=ALU.mult,
+            )
+
+        def turn_a(i, g):
+            if g == 0:
+                live["a_grouped", i] = work.tile([P, PASSES, P, PACK], BF16, name="a_grouped", align_bytes=64)
+                live["a_codes", i] = work.tile([P, PASSES, P], U32, name="a_codes", align_bytes=64)
+                live["a_scales", i] = work.tile([P, PASSES, P], U8, name="a_scales", align_bytes=64)
+            rows = live["a_nor", i]
+            turned = four_transposes([rows[:, (g * PACK + t) * P : (g * PACK + t + 1) * P] for t in range(PACK)])
+            nc.vector.tensor_copy(out=live["a_grouped", i][:, g], in_=turned[:].rearrange("p t r -> p r t"))
+
+        def values(i):
+            live["ret", i] = ps_plain.tile([P, D], F32, name="ret", tag="plain")
+            for g in range(PASSES):
+                nc.tensor.matmul_mx(
+                    out=live["ret", i][:],
+                    lhsT=live["a_codes", i][:, g, :].bitcast(FP8X4),
+                    lhsT_scale=live["a_scales", i][:, g, :],
+                    rhs=v_codes[:, g, :].bitcast(FP8X4),
+                    rhs_scale=v_scales[:, g, :],
+                    start=(g == 0),
+                    stop=(g == PASSES - 1),
+                )
+
+        def elu_clip(i):
+            live["clipped", i] = small.tile([P, D], F32, name="clipped")
+            nc.scalar.activation(out=live["clipped", i][:], in_=live["ret", i][:], func=ACT.Relu, scale=-1.0)
+
+        def elu_exp(i):
+            live["grown", i] = small.tile([P, D], F32, name="grown")
+            nc.scalar.activation(out=live["grown", i][:], in_=live["clipped", i][:], func=ACT.Exp, scale=-1.0)
+
+        def elu_store(i):
+            nc.vector.scalar_tensor_tensor(
+                out=result[:, i, :],
+                in0=live["grown", i][:],
+                scalar=-1.0,
+                in1=live["ret", i][:],
+                op0=ALU.add,
+                op1=ALU.max,
+            )
+            nc.sync.dma_start(out=out_tiles[:, i, :], in_=result[:, i, :])
+
+        def regroup_counting_attn(g):
+            live["c_grouped", g] = work.tile([P, NODES, PACK], BF16, name="c_grouped", align_bytes=64)
+            for engine_copy, cols in ((nc.vector.tensor_copy, slice(0, HALF)), (nc.scalar.copy, slice(HALF, NODES))):
+                engine_copy(
+                    out=live["c_grouped", g][:, cols, :].rearrange("p (w i) t -> p w t i", i=4),
+                    in_=c_raw[g][:, :, cols].rearrange("p t (w i) -> p w t i", i=4),
+                )
 
         def quantise_counting_attn(g):
             for c in range(CHUNKS):
-                c_grouped = c_stage.tile([P, BANK, PACK], BF16, align_bytes=64)
-                dst = c_grouped[:].rearrange("p (w i) t -> p w t i", i=4)
-                src = c_raw[g][:, :, c * BANK : (c + 1) * BANK].rearrange("p t (w i) -> p w t i", i=4)
-                if c == CHUNKS - 1:
-                    nc.scalar.copy(out=dst, in_=src)
-                else:
-                    nc.vector.tensor_copy(out=dst, in_=src)
+                cols = slice(c * BANK, (c + 1) * BANK)
                 nc.vector.quantize_mx(
-                    out=c_codes[:, g, c * BANK : (c + 1) * BANK].bitcast(FP8X4),
-                    scales=c_scales[:, g, c * BANK : (c + 1) * BANK],
-                    in_=c_grouped[:].rearrange("p w t -> p (w t)"),
+                    out=c_codes[:, g, cols].bitcast(FP8X4),
+                    scales=c_scales[:, g, cols],
+                    in_=live["c_grouped", g][:, cols, :].rearrange("p w t -> p (w t)"),
                 )
 
         def quantise_v():
             v_grouped = keep.tile([P, PASSES, D, PACK], BF16, align_bytes=64)
             nc.vector.tensor_copy(out=v_grouped[:], in_=v_raw[:].rearrange("p g t d -> p g d t"))
             for g in range(PASSES):
-                nc.vector.quantize_mx(
-                    out=v_codes[:, g, :].bitcast(FP8X4),
-                    scales=v_scales[:, g, :],
-                    in_=v_grouped[:, g].rearrange("p d t -> p (d t)"),
-                )
+                quantise(v_grouped, v_codes, v_scales, g)
 
-        def attend(i, e_codes, e_scales):
-            a_nomi = work.tile([P, CHUNKS, BANK], F32)
-            chunk_sum = small.tile([P, CHUNKS], F32)
-            for c in range(CHUNKS):
-                sums = ps_sums.tile([P, BANK], F32)
-                for g in range(PASSES):
-                    nc.tensor.matmul_mx(
-                        out=sums[:],
-                        lhsT=e_codes[:, g, :].bitcast(FP8X4),
-                        lhsT_scale=e_scales[:, g, :],
-                        rhs=c_codes[:, g, c * BANK : (c + 1) * BANK].bitcast(FP8X4),
-                        rhs_scale=c_scales[:, g, c * BANK : (c + 1) * BANK],
-                        start=(g == 0),
-                        stop=(g == PASSES - 1),
-                    )
-                nc.scalar.activation(
-                    out=a_nomi[:, c, :], in_=sums[:], func=ACT.Copy, accum_out=chunk_sum[:, c : c + 1]
-                )
-            unused = small.tile([P, CHUNKS], F32)
-            a_deno = small.tile([P, 1], F32)
-            nc.vector.tensor_scalar(
-                out=unused[:],
-                in0=chunk_sum[:],
-                scalar1=1.0,
-                scalar2=EPS,
-                op0=ALU.mult,
-                op1=ALU.add,
-                accum_out=a_deno[:],
-            )
-            inverse = small.tile([P, 1], F32)
-            nc.vector.reciprocal(out=inverse[:], in_=a_deno[:])
-            a_nor = work.tile([P, NODES], BF16)
-            nc.vector.tensor_scalar(
-                out=a_nor[:],
-                in0=a_nomi[:].rearrange("p c j -> p (c j)"),
-                scalar1=inverse[:, 0:1],
-                scalar2=None,
-                op0=ALU.mult,
-            )
-            a_codes = stage.tile([P, PASSES, P], U32, align_bytes=64)
-            a_scales = stage.tile([P, PASSES, P], U8, align_bytes=64)
-            turn_and_quantise(nc, stage, ps_turned, ident[:], a_nor, a_codes, a_scales)
-
-            ret = ps_out.tile([P, D], F32)
-            for g in range(PASSES):
-                nc.tensor.matmul_mx(
-                    out=ret[:],
-                    lhsT=a_codes[:, g, :].bitcast(FP8X4),
-                    lhsT_scale=a_scales[:, g, :],
-                    rhs=v_codes[:, g, :].bitcast(FP8X4),
-                    rhs_scale=v_scales[:, g, :],
-                    start=(g == 0),
-                    stop=(g == PASSES - 1),
-                )
-            negative = small.tile([P, D], F32)
-            nc.vector.tensor_scalar_min(out=negative[:], in0=ret[:], scalar1=0.0)
-            grown = small.tile([P, D], F32)
-            nc.scalar.activation(out=grown[:], in_=negative[:], func=ACT.Exp)
-            nc.vector.scalar_tensor_tensor(
-                out=result[:, i, :], in0=grown[:], scalar=-1.0, in1=ret[:], op0=ALU.add, op1=ALU.max
-            )
-            nc.sync.dma_start(out=out_tiles[:, i, :], in_=result[:, i, :])
-
-        quantised_e = []
-        for i in range(AHEAD):
-            quantised_e.append(softmax_numerator(i))
         for g in range(PASSES):
-            quantise_counting_attn(g)
+            turned = four_transposes([k_raw[:, g, t, :] for t in range(PACK)])
+            nc.vector.tensor_copy(out=kT[:, g * K_PASS : (g + 1) * K_PASS], in_=turned[:].rearrange("p t r -> p (t r)"))
+        for g in range(PASSES):
+            turned = four_transposes([q_raw[:, g * PACK + t, :] for t in range(PACK)])
+            nc.scalar.copy(out=qT[:, g * K_PASS : (g + 1) * K_PASS], in_=turned[:].rearrange("p t r -> p (t r)"))
+
+        def quantise_e(i, g):
+            quantise(live["e_grouped", i], live["e_codes", i], live["e_scales", i], g)
+
+        def logits_of(i):
+            for c in range(CHUNKS):
+                logits_chunk(i, c)
+            row_maximum(i)
+
+        logits_of(0)
+        regroup_counting_attn(0)
+        logits_of(1)
+        exponent(0)
+        quantise_counting_attn(0)
+        regroup_counting_attn(1)
+        for g in range(PASSES):
+            turn_e(0, g)
+        logits_of(2)
+        exponent(1)
+        quantise_counting_attn(1)
+        regroup_counting_attn(2)
+        for g in range(PASSES):
+            quantise_e(0, g)
+        for g in range(PASSES):
+            turn_e(1, g)
+        quantise_counting_attn(2)
+        for g in range(PASSES):
+            quantise_e(1, g)
         quantise_v()
-        for i in range(TILES):
-            if i + AHEAD < TILES:
-                quantised_e.append(softmax_numerator(i + AHEAD))
-            attend(i, quantised_e[i][0], quantised_e[i][1])
+
+        def on(i):
+            return 0 <= i < TILES
+
+        for a in range(TILES + 3):
+            if on(a - 3):
+                elu_store(a - 3)
+            if on(a + 2):
+                exponent(a + 2)
+            if on(a - 1):
+                normalise(a - 1)
+            for c in range(CHUNKS):
+                if on(a):
+                    counting_chunk(a, c)
+                if on(a + 3):
+                    logits_chunk(a + 3, c)
+            if on(a - 2):
+                values(a - 2)
+                elu_clip(a - 2)
+            if on(a + 3):
+                row_maximum(a + 3)
+            if on(a):
+                row_sum(a)
+            for g in range(PASSES):
+                if on(a + 2):
+                    turn_e(a + 2, g)
+                if on(a - 1):
+                    turn_a(a - 1, g)
+                if on(a + 2):
+                    quantise_e(a + 2, g)
+            if on(a - 2):
+                elu_exp(a - 2)
+            if on(a):
+                invert(a)
+            if on(a - 1):
+                for g in range(PASSES):
+                    quantise(live["a_grouped", a - 1], live["a_codes", a - 1], live["a_scales", a - 1], g)

@@ -22,6 +22,7 @@ PASSES = NODES // K_PASS
 BANK = 512
 CHUNKS = NODES // BANK
 HALF = NODES // 2
+PAIR = 2
 LOGIT_SCALE = 1.0 / (D ** 0.5)
 EPS = 1e-9
 
@@ -42,6 +43,8 @@ def tile_gkatlayer_pa_kernel(tc, q, k, counting_attn, v, out):
 
         ident = keep.tile([P, P], BF16)
         make_identity(nc, ident[:])
+        ident_words = keep.tile([P, P], F32)
+        make_identity(nc, ident_words[:])
 
         k_raw = keep.tile([P, PASSES, PACK, D], BF16)
         nc.sync.dma_start(out=k_raw[:], in_=k.rearrange("(g p t) d -> p g t d", p=P, t=PACK))
@@ -56,7 +59,10 @@ def tile_gkatlayer_pa_kernel(tc, q, k, counting_attn, v, out):
             )
             c_raw.append(c_rows)
         v_raw = keep.tile([P, PASSES, PACK, D], BF16)
-        nc.sync.dma_start(out=v_raw[:], in_=v.rearrange("(g t p) d -> p g t d", t=PACK, p=P))
+        nc.sync.dma_start(
+            out=v_raw[:].rearrange("p g (u e) d -> p (g u) (e d)", e=PAIR),
+            in_=v.rearrange("(gu p e) d -> p gu (e d)", p=P, e=PAIR),
+        )
 
         kT = keep.tile([P, NODES], BF16)
         qT = keep.tile([P, NODES], BF16)
@@ -75,12 +81,19 @@ def tile_gkatlayer_pa_kernel(tc, q, k, counting_attn, v, out):
                 nc.tensor.transpose(turned[:, t, :], blocks[t], ident[:])
             return turned
 
+        def turn_words(rows, g):
+            words = rows[:].bitcast(F32)
+            turned = ps_turned.tile([P, PAIR, P], F32, name="turned_words", tag="turned")
+            for u in range(PAIR):
+                w0 = (g * PAIR + u) * P
+                nc.tensor.transpose(turned[:, u, :], words[:, w0 : w0 + P], ident_words[:])
+            return turned[:].rearrange("p u r -> p r u")
+
+        def as_words(grouped, g):
+            return grouped[:, g, :].bitcast(F32).rearrange("p (r u) -> p r u", u=PAIR)
+
         def quantise(grouped, codes, scales, g):
-            nc.vector.quantize_mx(
-                out=codes[:, g, :].bitcast(FP8X4),
-                scales=scales[:, g, :],
-                in_=grouped[:, g].rearrange("p r t -> p (r t)"),
-            )
+            nc.vector.quantize_mx(out=codes[:, g, :].bitcast(FP8X4), scales=scales[:, g, :], in_=grouped[:, g, :])
 
         def logits_chunk(i, c):
             if c == 0:
@@ -122,12 +135,10 @@ def tile_gkatlayer_pa_kernel(tc, q, k, counting_attn, v, out):
 
         def turn_e(i, g):
             if g == 0:
-                live["e_grouped", i] = work.tile([P, PASSES, P, PACK], BF16, name="e_grouped", align_bytes=64)
+                live["e_grouped", i] = work.tile([P, PASSES, K_PASS], BF16, name="e_grouped", align_bytes=64)
                 live["e_codes", i] = work.tile([P, PASSES, P], U32, name="e_codes", bufs=3, align_bytes=64)
                 live["e_scales", i] = work.tile([P, PASSES, P], U8, name="e_scales", bufs=3, align_bytes=64)
-            rows = live["e_rows", i]
-            turned = four_transposes([rows[:, (g * PACK + t) * P : (g * PACK + t + 1) * P] for t in range(PACK)])
-            nc.scalar.copy(out=live["e_grouped", i][:, g], in_=turned[:].rearrange("p t r -> p r t"))
+            nc.scalar.copy(out=as_words(live["e_grouped", i], g), in_=turn_words(live["e_rows", i], g))
 
         def counting_chunk(i, c):
             if c == 0:
@@ -180,12 +191,10 @@ def tile_gkatlayer_pa_kernel(tc, q, k, counting_attn, v, out):
 
         def turn_a(i, g):
             if g == 0:
-                live["a_grouped", i] = work.tile([P, PASSES, P, PACK], BF16, name="a_grouped", align_bytes=64)
+                live["a_grouped", i] = work.tile([P, PASSES, K_PASS], BF16, name="a_grouped", align_bytes=64)
                 live["a_codes", i] = work.tile([P, PASSES, P], U32, name="a_codes", align_bytes=64)
                 live["a_scales", i] = work.tile([P, PASSES, P], U8, name="a_scales", align_bytes=64)
-            rows = live["a_nor", i]
-            turned = four_transposes([rows[:, (g * PACK + t) * P : (g * PACK + t + 1) * P] for t in range(PACK)])
-            nc.vector.tensor_copy(out=live["a_grouped", i][:, g], in_=turned[:].rearrange("p t r -> p r t"))
+            nc.vector.tensor_copy(out=as_words(live["a_grouped", i], g), in_=turn_words(live["a_nor", i], g))
 
         def values(i):
             live["ret", i] = ps_plain.tile([P, D], F32, name="ret", tag="plain")
@@ -237,14 +246,19 @@ def tile_gkatlayer_pa_kernel(tc, q, k, counting_attn, v, out):
                 )
 
         def quantise_v():
-            v_grouped = keep.tile([P, PASSES, D, PACK], BF16, align_bytes=64)
-            nc.vector.tensor_copy(out=v_grouped[:], in_=v_raw[:].rearrange("p g t d -> p g d t"))
+            v_grouped = keep.tile([P, PASSES, K_PASS], BF16, align_bytes=64)
+            nc.vector.tensor_copy(
+                out=v_grouped[:].rearrange("p g (d t) -> p g d t", t=PACK), in_=v_raw[:].rearrange("p g t d -> p g d t")
+            )
             for g in range(PASSES):
                 quantise(v_grouped, v_codes, v_scales, g)
 
         for g in range(PASSES):
             turned = four_transposes([k_raw[:, g, t, :] for t in range(PACK)])
-            nc.vector.tensor_copy(out=kT[:, g * K_PASS : (g + 1) * K_PASS], in_=turned[:].rearrange("p t r -> p (t r)"))
+            nc.vector.tensor_copy(
+                out=kT[:, g * K_PASS : (g + 1) * K_PASS].rearrange("d (u p e) -> d u p e", u=PAIR, e=PAIR),
+                in_=turned[:].rearrange("d (u e) p -> d u p e", e=PAIR),
+            )
         for g in range(PASSES):
             turned = four_transposes([q_raw[:, g * PACK + t, :] for t in range(PACK)])
             nc.scalar.copy(out=qT[:, g * K_PASS : (g + 1) * K_PASS], in_=turned[:].rearrange("p t r -> p (t r)"))

@@ -32,7 +32,6 @@ FLOPS = 2 * NODES * NODES * D + 2 * NODES * NODES * NODES + 2 * NODES * NODES * 
 def tile_gkatlayer_pa_kernel(tc, q, k, counting_attn, v, out):
     nc = tc.nc
     with ExitStack() as ctx:
-        ctx.enter_context(tc.manual_schedule())
         keep = ctx.enter_context(tc.tile_pool(name="keep", bufs=1))
         c_in = ctx.enter_context(tc.tile_pool(name="c_in", bufs=PASSES))
         work = ctx.enter_context(tc.tile_pool(name="work", bufs=2))

@@ -14,6 +14,7 @@ AX = mybir.AxisListType
 
 P = 128
 PACK = 4
+PAIR = 2
 K_PASS = P * PACK
 NODES = 1536
 D = 128
@@ -22,9 +23,15 @@ PASSES = NODES // K_PASS
 BANK = 512
 CHUNKS = NODES // BANK
 HALF = NODES // 2
-PAIR = 2
+RUN = 4
 LOGIT_SCALE = 1.0 / (D ** 0.5)
 EPS = 1e-9
+
+LOGITS_AHEAD = 3
+E_AHEAD = 2
+A_NOR_BEHIND = 1
+VALUES_BEHIND = 2
+STORE_BEHIND = 3
 
 FLOPS = 2 * NODES * NODES * D + 2 * NODES * NODES * NODES + 2 * NODES * NODES * D
 
@@ -33,36 +40,18 @@ def tile_gkatlayer_pa_kernel(tc, q, k, counting_attn, v, out):
     nc = tc.nc
     with ExitStack() as ctx:
         keep = ctx.enter_context(tc.tile_pool(name="keep", bufs=1))
-        c_in = ctx.enter_context(tc.tile_pool(name="c_in", bufs=PASSES))
         work = ctx.enter_context(tc.tile_pool(name="work", bufs=2))
-        small = ctx.enter_context(tc.tile_pool(name="small", bufs=4))
+        small = ctx.enter_context(tc.tile_pool(name="small", bufs=STORE_BEHIND + 1))
         ps_plain = ctx.enter_context(tc.psum_pool(name="ps_plain", bufs=2))
-        ps_sums = ctx.enter_context(tc.psum_pool(name="ps_sums", bufs=3))
-        ps_turned = ctx.enter_context(tc.psum_pool(name="ps_turned", bufs=3))
+        ps_sums = ctx.enter_context(tc.psum_pool(name="ps_sums", bufs=CHUNKS))
+        ps_turned = ctx.enter_context(tc.psum_pool(name="ps_turned", bufs=PASSES))
 
         ident = keep.tile([P, P], BF16)
-        make_identity(nc, ident[:])
         ident_words = keep.tile([P, P], F32)
-        make_identity(nc, ident_words[:])
-
         k_raw = keep.tile([P, PASSES, PACK, D], BF16)
-        nc.sync.dma_start(out=k_raw[:], in_=k.rearrange("(g p t) d -> p g t d", p=P, t=PACK))
         q_raw = keep.tile([P, TILES, D], BF16)
-        nc.sync.dma_start(out=q_raw[:], in_=q.rearrange("(p i) d -> p i d", i=TILES))
-        c_raw = []
-        for g in range(PASSES):
-            c_rows = c_in.tile([P, PACK, NODES], BF16)
-            nc.sync.dma_start(
-                out=c_rows[:],
-                in_=counting_attn[g * K_PASS : (g + 1) * K_PASS, :].rearrange("(p t) j -> p t j", t=PACK),
-            )
-            c_raw.append(c_rows)
+        c_raw = [keep.tile([P, PACK, NODES], BF16, name="c_raw%d" % g) for g in range(PASSES)]
         v_raw = keep.tile([P, PASSES, PACK, D], BF16)
-        nc.sync.dma_start(
-            out=v_raw[:].rearrange("p g (u e) d -> p (g u) (e d)", e=PAIR),
-            in_=v.rearrange("(gu p e) d -> p gu (e d)", p=P, e=PAIR),
-        )
-
         kT = keep.tile([P, NODES], BF16)
         qT = keep.tile([P, NODES], BF16)
         c_codes = keep.tile([P, PASSES, NODES], U32, align_bytes=64)
@@ -71,6 +60,19 @@ def tile_gkatlayer_pa_kernel(tc, q, k, counting_attn, v, out):
         v_scales = keep.tile([P, PASSES, D], U8, align_bytes=64)
         result = keep.tile([P, TILES, D], F32)
         out_tiles = out.rearrange("(p i) d -> p i d", i=TILES)
+
+        def load_inputs():
+            nc.sync.dma_start(out=k_raw[:], in_=k.rearrange("(g p t) d -> p g t d", p=P, t=PACK))
+            nc.sync.dma_start(out=q_raw[:], in_=q.rearrange("(p i) d -> p i d", i=TILES))
+            for g in range(PASSES):
+                nc.sync.dma_start(
+                    out=c_raw[g][:],
+                    in_=counting_attn[g * K_PASS : (g + 1) * K_PASS, :].rearrange("(p t) j -> p t j", t=PACK),
+                )
+            nc.sync.dma_start(
+                out=v_raw[:].rearrange("p g (u h) d -> p (g u) (h d)", h=PAIR),
+                in_=v.rearrange("(gu p h) d -> p gu (h d)", p=P, h=PAIR),
+            )
 
         live = {}
 
@@ -135,9 +137,12 @@ def tile_gkatlayer_pa_kernel(tc, q, k, counting_attn, v, out):
         def turn_e(i, g):
             if g == 0:
                 live["e_grouped", i] = work.tile([P, PASSES, K_PASS], BF16, name="e_grouped", align_bytes=64)
-                live["e_codes", i] = work.tile([P, PASSES, P], U32, name="e_codes", bufs=3, align_bytes=64)
-                live["e_scales", i] = work.tile([P, PASSES, P], U8, name="e_scales", bufs=3, align_bytes=64)
+                live["e_codes", i] = work.tile([P, PASSES, P], U32, name="e_codes", bufs=E_AHEAD + 1, align_bytes=64)
+                live["e_scales", i] = work.tile([P, PASSES, P], U8, name="e_scales", bufs=E_AHEAD + 1, align_bytes=64)
             nc.scalar.copy(out=as_words(live["e_grouped", i], g), in_=turn_words(live["e_rows", i], g))
+
+        def quantise_e(i, g):
+            quantise(live["e_grouped", i], live["e_codes", i], live["e_scales", i], g)
 
         def counting_chunk(i, c):
             if c == 0:
@@ -162,10 +167,10 @@ def tile_gkatlayer_pa_kernel(tc, q, k, counting_attn, v, out):
             )
 
         def row_sum(i):
-            unused = small.tile([P, CHUNKS], F32, name="unused")
+            unwanted = small.tile([P, CHUNKS], F32, name="unwanted")
             live["a_deno", i] = small.tile([P, 1], F32, name="a_deno")
             nc.vector.tensor_scalar(
-                out=unused[:],
+                out=unwanted[:],
                 in0=live["chunk_sum", i][:],
                 scalar1=1.0,
                 scalar2=EPS,
@@ -188,12 +193,15 @@ def tile_gkatlayer_pa_kernel(tc, q, k, counting_attn, v, out):
                 op0=ALU.mult,
             )
 
-        def turn_a(i, g):
+        def turn_a_nor(i, g):
             if g == 0:
                 live["a_grouped", i] = work.tile([P, PASSES, K_PASS], BF16, name="a_grouped", align_bytes=64)
                 live["a_codes", i] = work.tile([P, PASSES, P], U32, name="a_codes", align_bytes=64)
                 live["a_scales", i] = work.tile([P, PASSES, P], U8, name="a_scales", align_bytes=64)
             nc.vector.tensor_copy(out=as_words(live["a_grouped", i], g), in_=turn_words(live["a_nor", i], g))
+
+        def quantise_a_nor(i, g):
+            quantise(live["a_grouped", i], live["a_codes", i], live["a_scales", i], g)
 
         def values(i):
             live["ret", i] = ps_plain.tile([P, D], F32, name="ret", tag="plain")
@@ -231,8 +239,8 @@ def tile_gkatlayer_pa_kernel(tc, q, k, counting_attn, v, out):
             live["c_grouped", g] = work.tile([P, NODES, PACK], BF16, name="c_grouped", align_bytes=64)
             for engine_copy, cols in ((nc.vector.tensor_copy, slice(0, HALF)), (nc.scalar.copy, slice(HALF, NODES))):
                 engine_copy(
-                    out=live["c_grouped", g][:, cols, :].rearrange("p (w i) t -> p w t i", i=4),
-                    in_=c_raw[g][:, :, cols].rearrange("p t (w i) -> p w t i", i=4),
+                    out=live["c_grouped", g][:, cols, :].rearrange("p (w i) t -> p w t i", i=RUN),
+                    in_=c_raw[g][:, :, cols].rearrange("p t (w i) -> p w t i", i=RUN),
                 )
 
         def quantise_counting_attn(g):
@@ -252,78 +260,84 @@ def tile_gkatlayer_pa_kernel(tc, q, k, counting_attn, v, out):
             for g in range(PASSES):
                 quantise(v_grouped, v_codes, v_scales, g)
 
-        for g in range(PASSES):
-            turned = four_transposes([k_raw[:, g, t, :] for t in range(PACK)])
-            nc.vector.tensor_copy(
-                out=kT[:, g * K_PASS : (g + 1) * K_PASS].rearrange("d (u p e) -> d u p e", u=PAIR, e=PAIR),
-                in_=turned[:].rearrange("d (u e) p -> d u p e", e=PAIR),
-            )
-        for g in range(PASSES):
-            turned = four_transposes([q_raw[:, g * PACK + t, :] for t in range(PACK)])
-            nc.scalar.copy(out=qT[:, g * K_PASS : (g + 1) * K_PASS], in_=turned[:].rearrange("p t r -> p (t r)"))
-
-        def quantise_e(i, g):
-            quantise(live["e_grouped", i], live["e_codes", i], live["e_scales", i], g)
+        def turn_k_and_q():
+            for g in range(PASSES):
+                turned = four_transposes([k_raw[:, g, t, :] for t in range(PACK)])
+                nc.vector.tensor_copy(
+                    out=kT[:, g * K_PASS : (g + 1) * K_PASS].rearrange("d (u p h) -> d u p h", u=PAIR, h=PAIR),
+                    in_=turned[:].rearrange("d (u h) p -> d u p h", h=PAIR),
+                )
+            for g in range(PASSES):
+                turned = four_transposes([q_raw[:, g * PACK + t, :] for t in range(PACK)])
+                nc.scalar.copy(out=qT[:, g * K_PASS : (g + 1) * K_PASS], in_=turned[:].rearrange("p t r -> p (t r)"))
 
         def logits_of(i):
             for c in range(CHUNKS):
                 logits_chunk(i, c)
             row_maximum(i)
 
-        logits_of(0)
-        regroup_counting_attn(0)
-        logits_of(1)
-        exponent(0)
-        quantise_counting_attn(0)
-        regroup_counting_attn(1)
-        for g in range(PASSES):
-            turn_e(0, g)
-        logits_of(2)
-        exponent(1)
-        quantise_counting_attn(1)
-        regroup_counting_attn(2)
-        for g in range(PASSES):
-            quantise_e(0, g)
-        for g in range(PASSES):
-            turn_e(1, g)
-        quantise_counting_attn(2)
-        for g in range(PASSES):
-            quantise_e(1, g)
-        quantise_v()
+        def before_the_rounds():
+            make_identity(nc, ident[:])
+            make_identity(nc, ident_words[:])
+            load_inputs()
+            turn_k_and_q()
+            logits_of(0)
+            regroup_counting_attn(0)
+            logits_of(1)
+            exponent(0)
+            quantise_counting_attn(0)
+            regroup_counting_attn(1)
+            for g in range(PASSES):
+                turn_e(0, g)
+            logits_of(2)
+            exponent(1)
+            quantise_counting_attn(1)
+            regroup_counting_attn(2)
+            for g in range(PASSES):
+                quantise_e(0, g)
+            for g in range(PASSES):
+                turn_e(1, g)
+            quantise_counting_attn(2)
+            for g in range(PASSES):
+                quantise_e(1, g)
+            quantise_v()
+
+        with tc.manual_schedule():
+            before_the_rounds()
 
         def on(i):
             return 0 <= i < TILES
 
-        for a in range(TILES + 3):
-            if on(a - 3):
-                elu_store(a - 3)
-            if on(a + 2):
-                exponent(a + 2)
-            if on(a - 1):
-                normalise(a - 1)
+        for a in range(TILES + STORE_BEHIND):
+            if on(a - STORE_BEHIND):
+                elu_store(a - STORE_BEHIND)
+            if on(a + E_AHEAD):
+                exponent(a + E_AHEAD)
+            if on(a - A_NOR_BEHIND):
+                normalise(a - A_NOR_BEHIND)
             for c in range(CHUNKS):
                 if on(a):
                     counting_chunk(a, c)
-                if on(a + 3):
-                    logits_chunk(a + 3, c)
-            if on(a - 2):
-                values(a - 2)
-                elu_clip(a - 2)
-            if on(a + 3):
-                row_maximum(a + 3)
+                if on(a + LOGITS_AHEAD):
+                    logits_chunk(a + LOGITS_AHEAD, c)
+            if on(a - VALUES_BEHIND):
+                values(a - VALUES_BEHIND)
+                elu_clip(a - VALUES_BEHIND)
+            if on(a + LOGITS_AHEAD):
+                row_maximum(a + LOGITS_AHEAD)
             if on(a):
                 row_sum(a)
             for g in range(PASSES):
-                if on(a + 2):
-                    turn_e(a + 2, g)
-                if on(a - 1):
-                    turn_a(a - 1, g)
-                if on(a + 2):
-                    quantise_e(a + 2, g)
-            if on(a - 2):
-                elu_exp(a - 2)
+                if on(a + E_AHEAD):
+                    turn_e(a + E_AHEAD, g)
+                if on(a - A_NOR_BEHIND):
+                    turn_a_nor(a - A_NOR_BEHIND, g)
+                if on(a + E_AHEAD):
+                    quantise_e(a + E_AHEAD, g)
+            if on(a - VALUES_BEHIND):
+                elu_exp(a - VALUES_BEHIND)
             if on(a):
                 invert(a)
-            if on(a - 1):
+            if on(a - A_NOR_BEHIND):
                 for g in range(PASSES):
-                    quantise(live["a_grouped", a - 1], live["a_codes", a - 1], live["a_scales", a - 1], g)
+                    quantise_a_nor(a - A_NOR_BEHIND, g)

@@ -74,6 +74,9 @@ def tile_gkatlayer_pa_kernel(tc, q, k, counting_attn, v, out):
                 in_=v.rearrange("(gu p h) d -> p gu (h d)", p=P, h=PAIR),
             )
 
+        SCALAR_ALONE = (nc.scalar.copy, nc.scalar.copy, nc.scalar.copy)
+        SHARED = (nc.scalar.copy, nc.scalar.copy, nc.vector.tensor_copy)
+
         live = {}
 
         def four_transposes(blocks):
@@ -82,16 +85,36 @@ def tile_gkatlayer_pa_kernel(tc, q, k, counting_attn, v, out):
                 nc.tensor.transpose(turned[:, t, :], blocks[t], ident[:])
             return turned
 
-        def turn_words(rows, g):
-            words = rows[:].bitcast(F32)
-            turned = ps_turned.tile([P, PAIR, P], F32, name="turned_words", tag="turned")
-            for u in range(PAIR):
-                w0 = (g * PAIR + u) * P
-                nc.tensor.transpose(turned[:, u, :], words[:, w0 : w0 + P], ident_words[:])
-            return turned[:].rearrange("p u r -> p r u")
+        def turn(pieces, engines):
+            grouped = work.tile([P, PAIR * PASSES, K_PASS], BF16, name="grouped", align_bytes=64)
+            for s0 in range(0, len(pieces), PAIR):
+                bank = pieces[s0 : s0 + PAIR]
+                turned = ps_turned.tile([P, PAIR * PAIR, P], F32, name="turned_words", tag="turned")
+                for s, (rows, g) in enumerate(bank):
+                    words = rows[:].bitcast(F32)
+                    for u in range(PAIR):
+                        w0 = (g * PAIR + u) * P
+                        nc.tensor.transpose(turned[:, s * PAIR + u, :], words[:, w0 : w0 + P], ident_words[:])
+                engines[s0 // PAIR](
+                    out=grouped[:, s0 : s0 + len(bank), :].bitcast(F32).rearrange("p s (r u) -> p s r u", u=PAIR),
+                    in_=turned[:, : PAIR * len(bank), :].rearrange("p (s u) r -> p s r u", u=PAIR),
+                )
+            return grouped
 
-        def as_words(grouped, g):
-            return grouped[:, g, :].bitcast(F32).rearrange("p (r u) -> p r u", u=PAIR)
+        def quantise_turned(grouped, count):
+            codes = work.tile([P, PAIR * PASSES, P], U32, name="codes", bufs=E_AHEAD + 2, align_bytes=64)
+            scales = work.tile([P, PAIR * PASSES, P], U8, name="scales", bufs=E_AHEAD + 2, align_bytes=64)
+            for s0 in range(0, count, PAIR):
+                s1 = min(s0 + PAIR, count)
+                nc.vector.quantize_mx(
+                    out=codes[:, s0:s1, :].rearrange("p s r -> p (s r)").bitcast(FP8X4),
+                    scales=scales[:, s0:s1, :].rearrange("p s r -> p (s r)"),
+                    in_=grouped[:, s0:s1, :].rearrange("p s k -> p (s k)"),
+                )
+            return codes, scales
+
+        def pieces_of(name, i):
+            return [(live[name, i], g) for g in range(PASSES)]
 
         def quantise(grouped, codes, scales, g):
             nc.vector.quantize_mx(out=codes[:, g, :].bitcast(FP8X4), scales=scales[:, g, :], in_=grouped[:, g, :])
@@ -134,26 +157,17 @@ def tile_gkatlayer_pa_kernel(tc, q, k, counting_attn, v, out):
                 scale=1.0,
             )
 
-        def turn_e(i, g):
-            if g == 0:
-                live["e_grouped", i] = work.tile([P, PASSES, K_PASS], BF16, name="e_grouped", align_bytes=64)
-                live["e_codes", i] = work.tile([P, PASSES, P], U32, name="e_codes", bufs=E_AHEAD + 1, align_bytes=64)
-                live["e_scales", i] = work.tile([P, PASSES, P], U8, name="e_scales", bufs=E_AHEAD + 1, align_bytes=64)
-            nc.scalar.copy(out=as_words(live["e_grouped", i], g), in_=turn_words(live["e_rows", i], g))
-
-        def quantise_e(i, g):
-            quantise(live["e_grouped", i], live["e_codes", i], live["e_scales", i], g)
-
         def counting_chunk(i, c):
             if c == 0:
                 live["a_nomi", i] = work.tile([P, CHUNKS, BANK], F32, name="a_nomi")
                 live["chunk_sum", i] = small.tile([P, CHUNKS], F32, name="chunk_sum")
             sums = ps_sums.tile([P, BANK], F32, name="sums")
+            codes, scales, first = live["e_codes", i]
             for g in range(PASSES):
                 nc.tensor.matmul_mx(
                     out=sums[:],
-                    lhsT=live["e_codes", i][:, g, :].bitcast(FP8X4),
-                    lhsT_scale=live["e_scales", i][:, g, :],
+                    lhsT=codes[:, first + g, :].bitcast(FP8X4),
+                    lhsT_scale=scales[:, first + g, :],
                     rhs=c_codes[:, g, c * BANK : (c + 1) * BANK].bitcast(FP8X4),
                     rhs_scale=c_scales[:, g, c * BANK : (c + 1) * BANK],
                     start=(g == 0),
@@ -193,23 +207,14 @@ def tile_gkatlayer_pa_kernel(tc, q, k, counting_attn, v, out):
                 op0=ALU.mult,
             )
 
-        def turn_a_nor(i, g):
-            if g == 0:
-                live["a_grouped", i] = work.tile([P, PASSES, K_PASS], BF16, name="a_grouped", align_bytes=64)
-                live["a_codes", i] = work.tile([P, PASSES, P], U32, name="a_codes", align_bytes=64)
-                live["a_scales", i] = work.tile([P, PASSES, P], U8, name="a_scales", align_bytes=64)
-            nc.vector.tensor_copy(out=as_words(live["a_grouped", i], g), in_=turn_words(live["a_nor", i], g))
-
-        def quantise_a_nor(i, g):
-            quantise(live["a_grouped", i], live["a_codes", i], live["a_scales", i], g)
-
         def values(i):
             live["ret", i] = ps_plain.tile([P, D], F32, name="ret", tag="plain")
+            codes, scales, first = live["a_codes", i]
             for g in range(PASSES):
                 nc.tensor.matmul_mx(
                     out=live["ret", i][:],
-                    lhsT=live["a_codes", i][:, g, :].bitcast(FP8X4),
-                    lhsT_scale=live["a_scales", i][:, g, :],
+                    lhsT=codes[:, first + g, :].bitcast(FP8X4),
+                    lhsT_scale=scales[:, first + g, :],
                     rhs=v_codes[:, g, :].bitcast(FP8X4),
                     rhs_scale=v_scales[:, g, :],
                     start=(g == 0),
@@ -287,19 +292,15 @@ def tile_gkatlayer_pa_kernel(tc, q, k, counting_attn, v, out):
             exponent(0)
             quantise_counting_attn(0)
             regroup_counting_attn(1)
-            for g in range(PASSES):
-                turn_e(0, g)
+            grouped_0 = turn(pieces_of("e_rows", 0), SCALAR_ALONE)
             logits_of(2)
             exponent(1)
             quantise_counting_attn(1)
             regroup_counting_attn(2)
-            for g in range(PASSES):
-                quantise_e(0, g)
-            for g in range(PASSES):
-                turn_e(1, g)
+            live["e_codes", 0] = quantise_turned(grouped_0, PASSES) + (0,)
+            grouped_1 = turn(pieces_of("e_rows", 1), SCALAR_ALONE)
             quantise_counting_attn(2)
-            for g in range(PASSES):
-                quantise_e(1, g)
+            live["e_codes", 1] = quantise_turned(grouped_1, PASSES) + (0,)
             quantise_v()
 
         with tc.manual_schedule():
@@ -327,17 +328,16 @@ def tile_gkatlayer_pa_kernel(tc, q, k, counting_attn, v, out):
                 row_maximum(a + LOGITS_AHEAD)
             if on(a):
                 row_sum(a)
-            for g in range(PASSES):
-                if on(a + E_AHEAD):
-                    turn_e(a + E_AHEAD, g)
-                if on(a - A_NOR_BEHIND):
-                    turn_a_nor(a - A_NOR_BEHIND, g)
-                if on(a + E_AHEAD):
-                    quantise_e(a + E_AHEAD, g)
+            pieces = []
+            if on(a + E_AHEAD):
+                pieces = pieces + pieces_of("e_rows", a + E_AHEAD)
+            if on(a - A_NOR_BEHIND):
+                pieces = pieces + pieces_of("a_nor", a - A_NOR_BEHIND)
+            if pieces:
+                codes, scales = quantise_turned(turn(pieces, SHARED), len(pieces))
+                live["e_codes", a + E_AHEAD] = (codes, scales, 0)
+                live["a_codes", a - A_NOR_BEHIND] = (codes, scales, len(pieces) - PASSES)
             if on(a - VALUES_BEHIND):
                 elu_exp(a - VALUES_BEHIND)
             if on(a):
                 invert(a)
-            if on(a - A_NOR_BEHIND):
-                for g in range(PASSES):
-                    quantise_a_nor(a - A_NOR_BEHIND, g)

@@ -62,9 +62,14 @@ def tile_gkatlayer_pa_kernel(tc, q, k, counting_attn, v, out):
         out_tiles = out.rearrange("(p i) d -> p i d", i=TILES)
 
         def load_inputs():
-            nc.sync.dma_start(out=k_raw[:], in_=k.rearrange("(g p t) d -> p g t d", p=P, t=PACK))
-            nc.sync.dma_start(out=q_raw[:], in_=q.rearrange("(p i) d -> p i d", i=TILES))
+            k_passes = k.rearrange("(g p t) d -> p g t d", p=P, t=PACK)
+            q_tiles = q.rearrange("(p i) d -> p i d", i=TILES)
+            nc.sync.dma_start(out=k_raw[:, 0, :, :], in_=k_passes[:, 0, :, :])
+            nc.sync.dma_start(out=q_raw[:, 0:PACK, :], in_=q_tiles[:, 0:PACK, :])
+            nc.sync.dma_start(out=k_raw[:, 1:, :, :], in_=k_passes[:, 1:, :, :])
             for g in range(PASSES):
+                if g == 1:
+                    nc.sync.dma_start(out=q_raw[:, PACK:, :], in_=q_tiles[:, PACK:, :])
                 nc.sync.dma_start(
                     out=c_raw[g][:],
                     in_=counting_attn[g * K_PASS : (g + 1) * K_PASS, :].rearrange("(p t) j -> p t j", t=PACK),
@@ -76,6 +81,7 @@ def tile_gkatlayer_pa_kernel(tc, q, k, counting_attn, v, out):
 
         SCALAR_ALONE = (nc.scalar.copy, nc.scalar.copy, nc.scalar.copy)
         SHARED = (nc.scalar.copy, nc.scalar.copy, nc.vector.tensor_copy)
+        LAST = (nc.scalar.copy, nc.vector.tensor_copy, nc.scalar.copy)
 
         live = {}
 
@@ -85,27 +91,27 @@ def tile_gkatlayer_pa_kernel(tc, q, k, counting_attn, v, out):
                 nc.tensor.transpose(turned[:, t, :], blocks[t], ident[:])
             return turned
 
-        def turn(pieces, engines):
+        def turn(pieces, engines, in_bank=PAIR):
             grouped = work.tile([P, PAIR * PASSES, K_PASS], BF16, name="grouped", align_bytes=64)
-            for s0 in range(0, len(pieces), PAIR):
-                bank = pieces[s0 : s0 + PAIR]
+            for s0 in range(0, len(pieces), in_bank):
+                bank = pieces[s0 : s0 + in_bank]
                 turned = ps_turned.tile([P, PAIR * PAIR, P], F32, name="turned_words", tag="turned")
                 for s, (rows, g) in enumerate(bank):
                     words = rows[:].bitcast(F32)
                     for u in range(PAIR):
                         w0 = (g * PAIR + u) * P
                         nc.tensor.transpose(turned[:, s * PAIR + u, :], words[:, w0 : w0 + P], ident_words[:])
-                engines[s0 // PAIR](
+                engines[s0 // in_bank](
                     out=grouped[:, s0 : s0 + len(bank), :].bitcast(F32).rearrange("p s (r u) -> p s r u", u=PAIR),
                     in_=turned[:, : PAIR * len(bank), :].rearrange("p (s u) r -> p s r u", u=PAIR),
                 )
             return grouped
 
-        def quantise_turned(grouped, count):
+        def quantise_turned(grouped, count, at_once=PAIR):
             codes = work.tile([P, PAIR * PASSES, P], U32, name="codes", bufs=E_AHEAD + 2, align_bytes=64)
             scales = work.tile([P, PAIR * PASSES, P], U8, name="scales", bufs=E_AHEAD + 2, align_bytes=64)
-            for s0 in range(0, count, PAIR):
-                s1 = min(s0 + PAIR, count)
+            for s0 in range(0, count, at_once):
+                s1 = min(s0 + at_once, count)
                 nc.vector.quantize_mx(
                     out=codes[:, s0:s1, :].rearrange("p s r -> p (s r)").bitcast(FP8X4),
                     scales=scales[:, s0:s1, :].rearrange("p s r -> p (s r)"),
@@ -121,8 +127,8 @@ def tile_gkatlayer_pa_kernel(tc, q, k, counting_attn, v, out):
 
         def logits_chunk(i, c):
             if c == 0:
-                live["scaled", i] = work.tile([P, CHUNKS, BANK], F32, name="scaled")
-                live["chunk_max", i] = small.tile([P, CHUNKS], F32, name="chunk_max")
+                live["negated", i] = work.tile([P, CHUNKS, BANK], F32, name="negated")
+                live["chunk_min", i] = small.tile([P, CHUNKS], F32, name="chunk_min")
             logits = ps_plain.tile([P, BANK], F32, name="logits", tag="plain")
             nc.tensor.matmul(
                 out=logits[:],
@@ -132,29 +138,35 @@ def tile_gkatlayer_pa_kernel(tc, q, k, counting_attn, v, out):
                 stop=True,
             )
             nc.vector.tensor_scalar(
-                out=live["scaled", i][:, c, :],
+                out=live["negated", i][:, c, :],
                 in0=logits[:],
-                scalar1=LOGIT_SCALE,
+                scalar1=-LOGIT_SCALE,
                 scalar2=None,
                 op0=ALU.mult,
-                op1=ALU.max,
-                accum_out=live["chunk_max", i][:, c : c + 1],
+                op1=ALU.min,
+                accum_out=live["chunk_min", i][:, c : c + 1],
             )
 
         def row_maximum(i):
+            chunk_min = live["chunk_min", i]
             live["minus_max", i] = small.tile([P, 1], F32, name="minus_max")
-            nc.vector.tensor_reduce(
-                out=live["minus_max", i][:], in_=live["chunk_max", i][:], axis=AX.X, op=ALU.max, negate=True
+            nc.gpsimd.tensor_scalar(
+                out=live["minus_max", i][:],
+                in0=chunk_min[:, 0:1],
+                scalar1=chunk_min[:, 1:2],
+                scalar2=chunk_min[:, 2:3],
+                op0=ALU.min,
+                op1=ALU.min,
             )
 
         def exponent(i):
             live["e_rows", i] = work.tile([P, NODES], BF16, name="e_rows")
             nc.scalar.activation(
                 out=live["e_rows", i][:],
-                in_=live["scaled", i][:].rearrange("p c m -> p (c m)"),
+                in_=live["negated", i][:].rearrange("p c m -> p (c m)"),
                 func=ACT.Exp,
                 bias=live["minus_max", i][:, 0:1],
-                scale=1.0,
+                scale=-1.0,
             )
 
         def counting_chunk(i, c):
@@ -199,13 +211,15 @@ def tile_gkatlayer_pa_kernel(tc, q, k, counting_attn, v, out):
 
         def normalise(i):
             live["a_nor", i] = work.tile([P, NODES], BF16, name="a_nor")
-            nc.vector.tensor_scalar(
-                out=live["a_nor", i][:],
-                in0=live["a_nomi", i][:].rearrange("p c j -> p (c j)"),
-                scalar1=live["inverse", i][:, 0:1],
-                scalar2=None,
-                op0=ALU.mult,
-            )
+            parts = 1 if i < TILES - 1 else CHUNKS
+            for c in range(0, CHUNKS, CHUNKS // parts):
+                nc.vector.tensor_scalar(
+                    out=live["a_nor", i][:, c * BANK : (c + CHUNKS // parts) * BANK],
+                    in0=live["a_nomi", i][:, c : c + CHUNKS // parts, :].rearrange("p c j -> p (c j)"),
+                    scalar1=live["inverse", i][:, 0:1],
+                    scalar2=None,
+                    op0=ALU.mult,
+                )
 
         def values(i):
             live["ret", i] = ps_plain.tile([P, D], F32, name="ret", tag="plain")
@@ -265,16 +279,16 @@ def tile_gkatlayer_pa_kernel(tc, q, k, counting_attn, v, out):
             for g in range(PASSES):
                 quantise(v_grouped, v_codes, v_scales, g)
 
-        def turn_k_and_q():
-            for g in range(PASSES):
-                turned = four_transposes([k_raw[:, g, t, :] for t in range(PACK)])
-                nc.vector.tensor_copy(
-                    out=kT[:, g * K_PASS : (g + 1) * K_PASS].rearrange("d (u p h) -> d u p h", u=PAIR, h=PAIR),
-                    in_=turned[:].rearrange("d (u h) p -> d u p h", h=PAIR),
-                )
-            for g in range(PASSES):
-                turned = four_transposes([q_raw[:, g * PACK + t, :] for t in range(PACK)])
-                nc.scalar.copy(out=qT[:, g * K_PASS : (g + 1) * K_PASS], in_=turned[:].rearrange("p t r -> p (t r)"))
+        def turn_k(g, engine_copy):
+            turned = four_transposes([k_raw[:, g, t, :] for t in range(PACK)])
+            engine_copy(
+                out=kT[:, g * K_PASS : (g + 1) * K_PASS].rearrange("d (u p h) -> d u p h", u=PAIR, h=PAIR),
+                in_=turned[:].rearrange("d (u h) p -> d u p h", h=PAIR),
+            )
+
+        def turn_q(g, engine_copy):
+            turned = four_transposes([q_raw[:, g * PACK + t, :] for t in range(PACK)])
+            engine_copy(out=qT[:, g * K_PASS : (g + 1) * K_PASS], in_=turned[:].rearrange("p t r -> p (t r)"))
 
         def logits_of(i):
             for c in range(CHUNKS):
@@ -285,9 +299,13 @@ def tile_gkatlayer_pa_kernel(tc, q, k, counting_attn, v, out):
             make_identity(nc, ident[:])
             make_identity(nc, ident_words[:])
             load_inputs()
-            turn_k_and_q()
+            turn_k(0, nc.vector.tensor_copy)
+            turn_q(0, nc.scalar.copy)
+            turn_k(1, nc.scalar.copy)
+            turn_k(2, nc.scalar.copy)
             logits_of(0)
             regroup_counting_attn(0)
+            turn_q(1, nc.scalar.copy)
             logits_of(1)
             exponent(0)
             quantise_counting_attn(0)
@@ -299,6 +317,7 @@ def tile_gkatlayer_pa_kernel(tc, q, k, counting_attn, v, out):
             regroup_counting_attn(2)
             live["e_codes", 0] = quantise_turned(grouped_0, PASSES) + (0,)
             grouped_1 = turn(pieces_of("e_rows", 1), SCALAR_ALONE)
+            turn_q(2, nc.scalar.copy)
             quantise_counting_attn(2)
             live["e_codes", 1] = quantise_turned(grouped_1, PASSES) + (0,)
             quantise_v()
@@ -334,7 +353,9 @@ def tile_gkatlayer_pa_kernel(tc, q, k, counting_attn, v, out):
             if on(a - A_NOR_BEHIND):
                 pieces = pieces + pieces_of("a_nor", a - A_NOR_BEHIND)
             if pieces:
-                codes, scales = quantise_turned(turn(pieces, SHARED), len(pieces))
+                in_bank = 1 if a - A_NOR_BEHIND == TILES - 1 else PAIR
+                grouped = turn(pieces, SHARED if in_bank == PAIR else LAST, in_bank)
+                codes, scales = quantise_turned(grouped, len(pieces), in_bank)
                 live["e_codes", a + E_AHEAD] = (codes, scales, 0)
                 live["a_codes", a - A_NOR_BEHIND] = (codes, scales, len(pieces) - PASSES)
             if on(a - VALUES_BEHIND):

@@ -50,7 +50,10 @@ def tile_gkatlayer_pa_kernel(tc, q, k, counting_attn, v, out):
         ident_words = keep.tile([P, P], F32)
         k_raw = keep.tile([P, PASSES, PACK, D], BF16)
         q_raw = keep.tile([P, TILES, D], BF16)
-        c_raw = [keep.tile([P, PACK, NODES], BF16, name="c_raw%d" % g) for g in range(PASSES)]
+        c_raw = [
+            [keep.tile([P, PACK, NODES // pieces], BF16, name="c_raw%d%d" % (g, h)) for h in range(pieces)]
+            for g, pieces in ((0, 2), (1, 1), (2, 1))
+        ]
         v_raw = keep.tile([P, PASSES, PACK, D], BF16)
         kT = keep.tile([P, NODES], BF16)
         qT = keep.tile([P, NODES], BF16)
@@ -59,6 +62,7 @@ def tile_gkatlayer_pa_kernel(tc, q, k, counting_attn, v, out):
         v_codes = keep.tile([P, PASSES, D], U32, align_bytes=64)
         v_scales = keep.tile([P, PASSES, D], U8, align_bytes=64)
         result = keep.tile([P, TILES, D], F32)
+        chunk_sums = keep.tile([P, TILES, CHUNKS + 1], F32)
         out_tiles = out.rearrange("(p i) d -> p i d", i=TILES)
 
         def load_inputs():
@@ -70,10 +74,10 @@ def tile_gkatlayer_pa_kernel(tc, q, k, counting_attn, v, out):
             for g in range(PASSES):
                 if g == 1:
                     nc.sync.dma_start(out=q_raw[:, PACK:, :], in_=q_tiles[:, PACK:, :])
-                nc.sync.dma_start(
-                    out=c_raw[g][:],
-                    in_=counting_attn[g * K_PASS : (g + 1) * K_PASS, :].rearrange("(p t) j -> p t j", t=PACK),
-                )
+                rows = counting_attn[g * K_PASS : (g + 1) * K_PASS, :].rearrange("(p t) j -> p t j", t=PACK)
+                width = NODES // len(c_raw[g])
+                for h in reversed(range(len(c_raw[g]))):
+                    nc.sync.dma_start(out=c_raw[g][h][:], in_=rows[:, :, h * width : (h + 1) * width])
             nc.sync.dma_start(
                 out=v_raw[:].rearrange("p g (u h) d -> p (g u) (h d)", h=PAIR),
                 in_=v.rearrange("(gu p h) d -> p gu (h d)", p=P, h=PAIR),
@@ -81,7 +85,7 @@ def tile_gkatlayer_pa_kernel(tc, q, k, counting_attn, v, out):
 
         SCALAR_ALONE = (nc.scalar.copy, nc.scalar.copy, nc.scalar.copy)
         SHARED = (nc.scalar.copy, nc.scalar.copy, nc.vector.tensor_copy)
-        LAST = (nc.scalar.copy, nc.vector.tensor_copy, nc.scalar.copy)
+        LAST = (nc.vector.tensor_copy, nc.scalar.copy, nc.vector.tensor_copy)
 
         live = {}
 
@@ -172,7 +176,6 @@ def tile_gkatlayer_pa_kernel(tc, q, k, counting_attn, v, out):
         def counting_chunk(i, c):
             if c == 0:
                 live["a_nomi", i] = work.tile([P, CHUNKS, BANK], F32, name="a_nomi")
-                live["chunk_sum", i] = small.tile([P, CHUNKS], F32, name="chunk_sum")
             sums = ps_sums.tile([P, BANK], F32, name="sums")
             codes, scales, first = live["e_codes", i]
             for g in range(PASSES):
@@ -189,21 +192,12 @@ def tile_gkatlayer_pa_kernel(tc, q, k, counting_attn, v, out):
                 out=live["a_nomi", i][:, c, :],
                 in_=sums[:],
                 func=ACT.Copy,
-                accum_out=live["chunk_sum", i][:, c : c + 1],
+                accum_out=chunk_sums[:, i, c : c + 1],
             )
 
         def row_sum(i):
-            unwanted = small.tile([P, CHUNKS], F32, name="unwanted")
             live["a_deno", i] = small.tile([P, 1], F32, name="a_deno")
-            nc.vector.tensor_scalar(
-                out=unwanted[:],
-                in0=live["chunk_sum", i][:],
-                scalar1=1.0,
-                scalar2=EPS,
-                op0=ALU.mult,
-                op1=ALU.add,
-                accum_out=live["a_deno", i][:],
-            )
+            nc.vector.tensor_reduce(out=live["a_deno", i][:], in_=chunk_sums[:, i, :], axis=AX.X, op=ALU.add)
 
         def invert(i):
             live["inverse", i] = small.tile([P, 1], F32, name="inverse")
@@ -211,14 +205,21 @@ def tile_gkatlayer_pa_kernel(tc, q, k, counting_attn, v, out):
 
         def normalise(i):
             live["a_nor", i] = work.tile([P, NODES], BF16, name="a_nor")
-            parts = 1 if i < TILES - 1 else CHUNKS
-            for c in range(0, CHUNKS, CHUNKS // parts):
+            last = i == TILES - 1
+            for c0, c1 in ((0, 1), (1, 2)) if last else ((0, CHUNKS),):
                 nc.vector.tensor_scalar(
-                    out=live["a_nor", i][:, c * BANK : (c + CHUNKS // parts) * BANK],
-                    in0=live["a_nomi", i][:, c : c + CHUNKS // parts, :].rearrange("p c j -> p (c j)"),
+                    out=live["a_nor", i][:, c0 * BANK : c1 * BANK],
+                    in0=live["a_nomi", i][:, c0:c1, :].rearrange("p c j -> p (c j)"),
                     scalar1=live["inverse", i][:, 0:1],
                     scalar2=None,
                     op0=ALU.mult,
+                )
+            if last:
+                nc.scalar.activation(
+                    out=live["a_nor", i][:, (CHUNKS - 1) * BANK :],
+                    in_=live["a_nomi", i][:, CHUNKS - 1, :],
+                    func=ACT.Copy,
+                    scale=live["inverse", i][:, 0:1],
                 )
 
         def values(i):
@@ -256,10 +257,12 @@ def tile_gkatlayer_pa_kernel(tc, q, k, counting_attn, v, out):
 
         def regroup_counting_attn(g):
             live["c_grouped", g] = work.tile([P, NODES, PACK], BF16, name="c_grouped", align_bytes=64)
-            for engine_copy, cols in ((nc.vector.tensor_copy, slice(0, HALF)), (nc.scalar.copy, slice(HALF, NODES))):
+            for h, engine_copy in enumerate((nc.vector.tensor_copy, nc.scalar.copy)):
+                cols = slice(h * HALF, (h + 1) * HALF)
+                raw = c_raw[g][h][:] if len(c_raw[g]) == 2 else c_raw[g][0][:, :, cols]
                 engine_copy(
                     out=live["c_grouped", g][:, cols, :].rearrange("p (w i) t -> p w t i", i=RUN),
-                    in_=c_raw[g][:, :, cols].rearrange("p t (w i) -> p w t i", i=RUN),
+                    in_=raw.rearrange("p t (w i) -> p w t i", i=RUN),
                 )
 
         def quantise_counting_attn(g):
@@ -298,10 +301,11 @@ def tile_gkatlayer_pa_kernel(tc, q, k, counting_attn, v, out):
         def before_the_rounds():
             make_identity(nc, ident[:])
             make_identity(nc, ident_words[:])
+            nc.gpsimd.memset(chunk_sums[:, :, CHUNKS], EPS)
             load_inputs()
             turn_k(0, nc.vector.tensor_copy)
             turn_q(0, nc.scalar.copy)
-            turn_k(1, nc.scalar.copy)
+            turn_k(1, nc.vector.tensor_copy)
             turn_k(2, nc.scalar.copy)
             logits_of(0)
             regroup_counting_attn(0)

from contextlib import ExitStack

import concourse.mybir as mybir
from concourse.masks import make_identity

F32 = mybir.dt.float32
BF16 = mybir.dt.bfloat16
U32 = mybir.dt.uint32
U8 = mybir.dt.uint8
FP8X4 = mybir.dt.float8_e4m3fn_x4
ACT = mybir.ActivationFunctionType
ALU = mybir.AluOpType
AX = mybir.AxisListType

P = 128
PACK = 4
PAIR = 2
K_PASS = P * PACK
NODES = 1536
D = 128
TILES = NODES // P
PASSES = NODES // K_PASS
BANK = 512
CHUNKS = NODES // BANK
HALF = NODES // 2
RUN = 4
LOGIT_SCALE = 1.0 / (D ** 0.5)
EPS = 1e-9

LOGITS_AHEAD = 3
E_AHEAD = 2
A_NOR_BEHIND = 1
VALUES_BEHIND = 2
STORE_BEHIND = 3

FLOPS = 2 * NODES * NODES * D + 2 * NODES * NODES * NODES + 2 * NODES * NODES * D


def tile_gkatlayer_pa_kernel(tc, q, k, counting_attn, v, out):
    nc = tc.nc
    with ExitStack() as ctx:
        keep = ctx.enter_context(tc.tile_pool(name="keep", bufs=1))
        work = ctx.enter_context(tc.tile_pool(name="work", bufs=2))
        small = ctx.enter_context(tc.tile_pool(name="small", bufs=STORE_BEHIND + 1))
        ps_plain = ctx.enter_context(tc.psum_pool(name="ps_plain", bufs=2))
        ps_sums = ctx.enter_context(tc.psum_pool(name="ps_sums", bufs=CHUNKS))
        ps_turned = ctx.enter_context(tc.psum_pool(name="ps_turned", bufs=PASSES))

        ident = keep.tile([P, P], BF16)
        ident_words = keep.tile([P, P], F32)
        k_raw = keep.tile([P, PASSES, PACK, D], BF16)
        q_raw = keep.tile([P, TILES, D], BF16)
        c_raw = [
            [keep.tile([P, PACK, NODES // pieces], BF16, name="c_raw%d%d" % (g, h)) for h in range(pieces)]
            for g, pieces in ((0, 2), (1, 1), (2, 1))
        ]
        v_raw = keep.tile([P, PASSES, PACK, D], BF16)
        kT = keep.tile([P, NODES], BF16)
        qT = keep.tile([P, NODES], BF16)
        c_codes = keep.tile([P, PASSES, NODES], U32, align_bytes=64)
        c_scales = keep.tile([P, PASSES, NODES], U8, align_bytes=64)
        v_codes = keep.tile([P, PASSES, D], U32, align_bytes=64)
        v_scales = keep.tile([P, PASSES, D], U8, align_bytes=64)
        result = keep.tile([P, TILES, D], F32)
        chunk_sums = keep.tile([P, TILES, CHUNKS + 1], F32)
        out_tiles = out.rearrange("(p i) d -> p i d", i=TILES)

        def load_inputs():
            k_passes = k.rearrange("(g p t) d -> p g t d", p=P, t=PACK)
            q_tiles = q.rearrange("(p i) d -> p i d", i=TILES)
            nc.sync.dma_start(out=k_raw[:, 0, :, :], in_=k_passes[:, 0, :, :])
            nc.sync.dma_start(out=q_raw[:, 0:PACK, :], in_=q_tiles[:, 0:PACK, :])
            nc.sync.dma_start(out=k_raw[:, 1:, :, :], in_=k_passes[:, 1:, :, :])
            for g in range(PASSES):
                if g == 1:
                    nc.sync.dma_start(out=q_raw[:, PACK:, :], in_=q_tiles[:, PACK:, :])
                rows = counting_attn[g * K_PASS : (g + 1) * K_PASS, :].rearrange("(p t) j -> p t j", t=PACK)
                width = NODES // len(c_raw[g])
                for h in reversed(range(len(c_raw[g]))):
                    nc.sync.dma_start(out=c_raw[g][h][:], in_=rows[:, :, h * width : (h + 1) * width])
            nc.sync.dma_start(
                out=v_raw[:].rearrange("p g (u h) d -> p (g u) (h d)", h=PAIR),
                in_=v.rearrange("(gu p h) d -> p gu (h d)", p=P, h=PAIR),
            )

        SCALAR_ALONE = (nc.scalar.copy, nc.scalar.copy, nc.scalar.copy)
        SHARED = (nc.scalar.copy, nc.scalar.copy, nc.vector.tensor_copy)
        LAST = (nc.vector.tensor_copy, nc.scalar.copy, nc.vector.tensor_copy)

        live = {}

        def four_transposes(blocks):
            turned = ps_turned.tile([P, PACK, P], BF16, name="turned")
            for t in range(PACK):
                nc.tensor.transpose(turned[:, t, :], blocks[t], ident[:])
            return turned

        def turn(pieces, engines, in_bank=PAIR):
            grouped = work.tile([P, PAIR * PASSES, K_PASS], BF16, name="grouped", align_bytes=64)
            for s0 in range(0, len(pieces), in_bank):
                bank = pieces[s0 : s0 + in_bank]
                turned = ps_turned.tile([P, PAIR * PAIR, P], F32, name="turned_words", tag="turned")
                for s, (rows, g) in enumerate(bank):
                    words = rows[:].bitcast(F32)
                    for u in range(PAIR):
                        w0 = (g * PAIR + u) * P
                        nc.tensor.transpose(turned[:, s * PAIR + u, :], words[:, w0 : w0 + P], ident_words[:])
                engines[s0 // in_bank](
                    out=grouped[:, s0 : s0 + len(bank), :].bitcast(F32).rearrange("p s (r u) -> p s r u", u=PAIR),
                    in_=turned[:, : PAIR * len(bank), :].rearrange("p (s u) r -> p s r u", u=PAIR),
                )
            return grouped

        def quantise_turned(grouped, count, at_once=PAIR):
            codes = work.tile([P, PAIR * PASSES, P], U32, name="codes", bufs=E_AHEAD + 2, align_bytes=64)
            scales = work.tile([P, PAIR * PASSES, P], U8, name="scales", bufs=E_AHEAD + 2, align_bytes=64)
            for s0 in range(0, count, at_once):
                s1 = min(s0 + at_once, count)
                nc.vector.quantize_mx(
                    out=codes[:, s0:s1, :].rearrange("p s r -> p (s r)").bitcast(FP8X4),
                    scales=scales[:, s0:s1, :].rearrange("p s r -> p (s r)"),
                    in_=grouped[:, s0:s1, :].rearrange("p s k -> p (s k)"),
                )
            return codes, scales

        def pieces_of(name, i):
            return [(live[name, i], g) for g in range(PASSES)]

        def quantise(grouped, codes, scales, g):
            nc.vector.quantize_mx(out=codes[:, g, :].bitcast(FP8X4), scales=scales[:, g, :], in_=grouped[:, g, :])

        def logits_chunk(i, c):
            if c == 0:
                live["negated", i] = work.tile([P, CHUNKS, BANK], F32, name="negated")
                live["chunk_min", i] = small.tile([P, CHUNKS], F32, name="chunk_min")
            logits = ps_plain.tile([P, BANK], F32, name="logits", tag="plain")
            nc.tensor.matmul(
                out=logits[:],
                lhsT=qT[:, i * P : (i + 1) * P],
                rhs=kT[:, c * BANK : (c + 1) * BANK],
                start=True,
                stop=True,
            )
            nc.vector.tensor_scalar(
                out=live["negated", i][:, c, :],
                in0=logits[:],
                scalar1=-LOGIT_SCALE,
                scalar2=None,
                op0=ALU.mult,
                op1=ALU.min,
                accum_out=live["chunk_min", i][:, c : c + 1],
            )

        def row_maximum(i):
            chunk_min = live["chunk_min", i]
            live["minus_max", i] = small.tile([P, 1], F32, name="minus_max")
            nc.gpsimd.tensor_scalar(
                out=live["minus_max", i][:],
                in0=chunk_min[:, 0:1],
                scalar1=chunk_min[:, 1:2],
                scalar2=chunk_min[:, 2:3],
                op0=ALU.min,
                op1=ALU.min,
            )

        def exponent(i):
            live["e_rows", i] = work.tile([P, NODES], BF16, name="e_rows")
            nc.scalar.activation(
                out=live["e_rows", i][:],
                in_=live["negated", i][:].rearrange("p c m -> p (c m)"),
                func=ACT.Exp,
                bias=live["minus_max", i][:, 0:1],
                scale=-1.0,
            )

        def counting_chunk(i, c):
            if c == 0:
                live["a_nomi", i] = work.tile([P, CHUNKS, BANK], F32, name="a_nomi")
            sums = ps_sums.tile([P, BANK], F32, name="sums")
            codes, scales, first = live["e_codes", i]
            for g in range(PASSES):
                nc.tensor.matmul_mx(
                    out=sums[:],
                    lhsT=codes[:, first + g, :].bitcast(FP8X4),
                    lhsT_scale=scales[:, first + g, :],
                    rhs=c_codes[:, g, c * BANK : (c + 1) * BANK].bitcast(FP8X4),
                    rhs_scale=c_scales[:, g, c * BANK : (c + 1) * BANK],
                    start=(g == 0),
                    stop=(g == PASSES - 1),
                )
            nc.scalar.activation(
                out=live["a_nomi", i][:, c, :],
                in_=sums[:],
                func=ACT.Copy,
                accum_out=chunk_sums[:, i, c : c + 1],
            )

        def row_sum(i):
            live["a_deno", i] = small.tile([P, 1], F32, name="a_deno")
            nc.vector.tensor_reduce(out=live["a_deno", i][:], in_=chunk_sums[:, i, :], axis=AX.X, op=ALU.add)

        def invert(i):
            live["inverse", i] = small.tile([P, 1], F32, name="inverse")
            nc.vector.reciprocal(out=live["inverse", i][:], in_=live["a_deno", i][:])

        def normalise(i):
            live["a_nor", i] = work.tile([P, NODES], BF16, name="a_nor")
            last = i == TILES - 1
            for c0, c1 in ((0, 1), (1, 2)) if last else ((0, CHUNKS),):
                nc.vector.tensor_scalar(
                    out=live["a_nor", i][:, c0 * BANK : c1 * BANK],
                    in0=live["a_nomi", i][:, c0:c1, :].rearrange("p c j -> p (c j)"),
                    scalar1=live["inverse", i][:, 0:1],
                    scalar2=None,
                    op0=ALU.mult,
                )
            if last:
                nc.scalar.activation(
                    out=live["a_nor", i][:, (CHUNKS - 1) * BANK :],
                    in_=live["a_nomi", i][:, CHUNKS - 1, :],
                    func=ACT.Copy,
                    scale=live["inverse", i][:, 0:1],
                )

        def values(i):
            live["ret", i] = ps_plain.tile([P, D], F32, name="ret", tag="plain")
            codes, scales, first = live["a_codes", i]
            for g in range(PASSES):
                nc.tensor.matmul_mx(
                    out=live["ret", i][:],
                    lhsT=codes[:, first + g, :].bitcast(FP8X4),
                    lhsT_scale=scales[:, first + g, :],
                    rhs=v_codes[:, g, :].bitcast(FP8X4),
                    rhs_scale=v_scales[:, g, :],
                    start=(g == 0),
                    stop=(g == PASSES - 1),
                )

        def elu_clip(i):
            live["clipped", i] = small.tile([P, D], F32, name="clipped")
            nc.scalar.activation(out=live["clipped", i][:], in_=live["ret", i][:], func=ACT.Relu, scale=-1.0)

        def elu_exp(i):
            live["grown", i] = small.tile([P, D], F32, name="grown")
            nc.scalar.activation(out=live["grown", i][:], in_=live["clipped", i][:], func=ACT.Exp, scale=-1.0)

        def elu_store(i):
            nc.vector.scalar_tensor_tensor(
                out=result[:, i, :],
                in0=live["grown", i][:],
                scalar=-1.0,
                in1=live["ret", i][:],
                op0=ALU.add,
                op1=ALU.max,
            )
            nc.sync.dma_start(out=out_tiles[:, i, :], in_=result[:, i, :])

        def regroup_counting_attn(g):
            live["c_grouped", g] = work.tile([P, NODES, PACK], BF16, name="c_grouped", align_bytes=64)
            for h, engine_copy in enumerate((nc.vector.tensor_copy, nc.scalar.copy)):
                cols = slice(h * HALF, (h + 1) * HALF)
                raw = c_raw[g][h][:] if len(c_raw[g]) == 2 else c_raw[g][0][:, :, cols]
                engine_copy(
                    out=live["c_grouped", g][:, cols, :].rearrange("p (w i) t -> p w t i", i=RUN),
                    in_=raw.rearrange("p t (w i) -> p w t i", i=RUN),
                )

        def quantise_counting_attn(g):
            for c in range(CHUNKS):
                cols = slice(c * BANK, (c + 1) * BANK)
                nc.vector.quantize_mx(
                    out=c_codes[:, g, cols].bitcast(FP8X4),
                    scales=c_scales[:, g, cols],
                    in_=live["c_grouped", g][:, cols, :].rearrange("p w t -> p (w t)"),
                )

        def quantise_v():
            v_grouped = keep.tile([P, PASSES, K_PASS], BF16, align_bytes=64)
            nc.vector.tensor_copy(
                out=v_grouped[:].rearrange("p g (d t) -> p g d t", t=PACK), in_=v_raw[:].rearrange("p g t d -> p g d t")
            )
            for g in range(PASSES):
                quantise(v_grouped, v_codes, v_scales, g)

        def turn_k(g, engine_copy):
            turned = four_transposes([k_raw[:, g, t, :] for t in range(PACK)])
            engine_copy(
                out=kT[:, g * K_PASS : (g + 1) * K_PASS].rearrange("d (u p h) -> d u p h", u=PAIR, h=PAIR),
                in_=turned[:].rearrange("d (u h) p -> d u p h", h=PAIR),
            )

        def turn_q(g, engine_copy):
            turned = four_transposes([q_raw[:, g * PACK + t, :] for t in range(PACK)])
            engine_copy(out=qT[:, g * K_PASS : (g + 1) * K_PASS], in_=turned[:].rearrange("p t r -> p (t r)"))

        def logits_of(i):
            for c in range(CHUNKS):
                logits_chunk(i, c)
            row_maximum(i)

        def before_the_rounds():
            make_identity(nc, ident[:])
            make_identity(nc, ident_words[:])
            nc.gpsimd.memset(chunk_sums[:, :, CHUNKS], EPS)
            load_inputs()
            turn_k(0, nc.vector.tensor_copy)
            turn_q(0, nc.scalar.copy)
            turn_k(1, nc.vector.tensor_copy)
            turn_k(2, nc.scalar.copy)
            logits_of(0)
            regroup_counting_attn(0)
            turn_q(1, nc.scalar.copy)
            logits_of(1)
            exponent(0)
            quantise_counting_attn(0)
            regroup_counting_attn(1)
            grouped_0 = turn(pieces_of("e_rows", 0), SCALAR_ALONE)
            logits_of(2)
            exponent(1)
            quantise_counting_attn(1)
            regroup_counting_attn(2)
            live["e_codes", 0] = quantise_turned(grouped_0, PASSES) + (0,)
            grouped_1 = turn(pieces_of("e_rows", 1), SCALAR_ALONE)
            turn_q(2, nc.scalar.copy)
            quantise_counting_attn(2)
            live["e_codes", 1] = quantise_turned(grouped_1, PASSES) + (0,)
            quantise_v()

        with tc.manual_schedule():
            before_the_rounds()

        def on(i):
            return 0 <= i < TILES

        for a in range(TILES + STORE_BEHIND):
            if on(a - STORE_BEHIND):
                elu_store(a - STORE_BEHIND)
            if on(a + E_AHEAD):
                exponent(a + E_AHEAD)
            if on(a - A_NOR_BEHIND):
                normalise(a - A_NOR_BEHIND)
            for c in range(CHUNKS):
                if on(a):
                    counting_chunk(a, c)
                if on(a + LOGITS_AHEAD):
                    logits_chunk(a + LOGITS_AHEAD, c)
            if on(a - VALUES_BEHIND):
                values(a - VALUES_BEHIND)
                elu_clip(a - VALUES_BEHIND)
            if on(a + LOGITS_AHEAD):
                row_maximum(a + LOGITS_AHEAD)
            if on(a):
                row_sum(a)
            pieces = []
            if on(a + E_AHEAD):
                pieces = pieces + pieces_of("e_rows", a + E_AHEAD)
            if on(a - A_NOR_BEHIND):
                pieces = pieces + pieces_of("a_nor", a - A_NOR_BEHIND)
            if pieces:
                in_bank = 1 if a - A_NOR_BEHIND == TILES - 1 else PAIR
                grouped = turn(pieces, SHARED if in_bank == PAIR else LAST, in_bank)
                codes, scales = quantise_turned(grouped, len(pieces), in_bank)
                live["e_codes", a + E_AHEAD] = (codes, scales, 0)
                live["a_codes", a - A_NOR_BEHIND] = (codes, scales, len(pieces) - PASSES)
            if on(a - VALUES_BEHIND):
                elu_exp(a - VALUES_BEHIND)
            if on(a):
                invert(a)
